import numpy as np
import ml_dtypes


def mxq(x, axis, fmt="e4m3"):
    dtype, down = {"e4m3": (ml_dtypes.float8_e4m3fn, 7), "e5m2": (ml_dtypes.float8_e5m2, 14)}[fmt]
    v = np.moveaxis(np.asarray(x, np.float32).astype(ml_dtypes.bfloat16).astype(np.float64), axis, -1)
    blocks = v.reshape(v.shape[:-1] + (-1, 32))
    amax = np.abs(blocks).max(-1, keepdims=True)
    byte = np.maximum(np.where(amax > 0, np.frexp(amax)[1] - 1 + 127, 0) - down, 1)
    scale = np.exp2(byte - 127.0)
    codes = (blocks / scale).astype(np.float32).astype(dtype).astype(np.float64)
    return np.moveaxis((codes * scale).reshape(v.shape), -1, axis)


WIDE = False


def mx_kscale(k):
    if not WIDE:
        return np.ones(k)
    levels = np.array([10, -10, 5, -5, 0])
    if k % 512:
        return np.exp2(np.random.permutation(np.resize(levels, k // 32))).repeat(32)
    a = np.empty((k // 512, 16))
    for p in range(k // 512):
        a[p, :8] = np.random.permutation(np.resize(levels, 8))
        for g in range(8):
            far = levels[np.abs(levels - a[p, g]) >= 10]
            a[p, g + 8] = far[np.random.randint(len(far))]
    return np.exp2(a.ravel()).repeat(32)


BF16 = ml_dtypes.bfloat16


def bf(x):
    return np.asarray(x, np.float32).astype(BF16)


def f64(x):
    return np.asarray(x).astype(np.float64)


B, H = 512, 1024
K = 2 * H
BETA_SHIFT = 1.0
LN_EPS = 1e-5
BAG_EPS = 1e-6


def setup_inputs():
    s = mx_kscale(H)
    r_main = np.random.uniform(0.5, 1.1, (B, 1))
    r_branch = np.random.uniform(0.5, 1.1, (B, 1))
    w_mb = np.random.standard_normal((K, H)) / np.sqrt(K)
    w_mb[H:] = w_mb[H:] / s[:, None]
    return {"main": bf(np.random.standard_normal((B, H)) * r_main),
            "branch": bf(np.random.standard_normal((B, H)) * r_branch * s),
            "o": bf(1.0 - np.random.random((B, 1)) * np.random.uniform(0.2, 0.8, (B, H))),
            "is_bag": bf(np.random.random((B, 1))),
            "W_mb": bf(w_mb),
            "b_mb": bf(np.random.standard_normal(H) * 0.3),
            "W_b": bf(np.random.standard_normal((H, H)) * 2.0 / np.sqrt(H) / s[:, None]),
            "b_b": bf(np.random.standard_normal(H) * 0.3),
            "ln_g": bf(1.0 + 0.1 * np.random.standard_normal(H)),
            "ln_b": bf(0.1 * np.random.standard_normal(H))}


def reference(main, branch, o, is_bag, W_mb, b_mb, W_b, b_b, ln_g, ln_b):
    main, is_bag = f64(main), f64(is_bag)
    mbq = mxq(np.concatenate([main, f64(branch)], axis=-1), 1, "e4m3")
    weight_b = np.maximum((mbq @ mxq(f64(W_mb), 0, "e4m3")) + f64(b_mb), 0.0)
    h_m = weight_b * ((mbq[:, H:] @ mxq(f64(W_b), 0, "e4m3")) + f64(b_b))
    em_norm = np.sqrt((main ** 2).sum(-1))
    hm_norm = np.sqrt((h_m ** 2).sum(-1))
    hm_norm = np.where(hm_norm == 0, np.ones_like(hm_norm), hm_norm)
    alpha = np.minimum(em_norm / (hm_norm + BAG_EPS) * BETA_SHIFT, 1.0)[:, None]
    pre = alpha * h_m + main
    mu = pre.mean(-1, keepdims=True)
    var = ((pre - mu) ** 2).mean(-1, keepdims=True)
    emb = (pre - mu) / np.sqrt(var + LN_EPS) * f64(ln_g) + f64(ln_b)
    shift_c = emb * is_bag + main * (1.0 - is_bag)
    h = f64(o) * np.tanh(shift_c)
    return h, shift_c

@@ -1,0 +1,413 @@
+from contextlib import ExitStack
+
+import concourse.mybir as mybir
+from concourse.masks import make_identity
+
+F32 = mybir.dt.float32
+BF16 = mybir.dt.bfloat16
+U32 = mybir.dt.uint32
+U8 = mybir.dt.uint8
+FP8X4 = mybir.dt.float8_e4m3fn_x4
+ACT = mybir.ActivationFunctionType
+ALU = mybir.AluOpType
+
+P = 128
+B = 512
+H = 1024
+RT = B // P
+HT = H // P
+FLOPS = 2 * B * (2 * H) * H + 2 * B * H * H
+SCALAR_UNITS = ((0, 1), (1, 1), (2, 1), (3, 1), (5, 1))
+PE_BLEND = (0, 1, 2)
+
+
+def tile_bag_lstm_pb_kernel(tc, main, branch, o, is_bag, W_mb, b_mb, W_b, b_b, ln_g, ln_b, out_0, out_1):
+    nc = tc.nc
+    with ExitStack() as ctx:
+        keep = ctx.enter_context(tc.tile_pool(name="keep", bufs=1))
+        rawp = ctx.enter_context(tc.tile_pool(name="rawp", bufs=4))
+        grpp = ctx.enter_context(tc.tile_pool(name="grpp", bufs=4))
+        work = ctx.enter_context(tc.tile_pool(name="work", bufs=2))
+        small = ctx.enter_context(tc.tile_pool(name="small", bufs=4))
+        psum = ctx.enter_context(tc.psum_pool(name="psum", bufs=1))
+        ctx.enter_context(tc.manual_schedule())
+
+        def bank(i, shape, name):
+            return psum.tile(shape, F32, tag="bank%d" % i, name=name)
+
+        ident = keep.tile([P, P], F32, name="ident")
+        ident_bf = keep.tile([P, P], BF16, name="ident_bf")
+        vecs_bf = keep.tile([P, P], BF16, name="vecs_bf")
+        vecs_f = keep.tile([P, P], F32, name="vecs_f")
+        vec = keep.tile([P, 2 * HT + RT], F32, name="vec")
+        one1 = keep.tile([P, 1], F32, name="one1")
+        eps_ln = keep.tile([P, 1], F32, name="eps_ln")
+        eps_bag = keep.tile([P, 1], F32, name="eps_bag")
+        warm = keep.tile([P, 2], F32, name="warm")
+        brow = keep.tile([P, H], BF16, name="brow")
+        srow = keep.tile([P, B], BF16, name="srow")
+        oms = keep.tile([P, RT], F32, name="oms")
+        main_sb = keep.tile([P, RT, H], BF16, name="main_sb")
+        branch_sb = keep.tile([P, RT, H], BF16, name="branch_sb")
+        o_sb = keep.tile([P, RT, H], BF16, name="o_sb")
+        gb = keep.tile([P, 2 * H], BF16, name="gb")
+        g_bc = gb[:, 0:H]
+        b_bc = gb[:, H:2 * H]
+        q3 = keep.tile([P, H], F32, name="q3")
+        dneg = [keep.tile([P, P], BF16, name="dneg%d" % r) for r in PE_BLEND]
+        ags = [keep.tile([P, 2 * B], F32, name="ag%d" % c, align_bytes=64) for c in range(4)]
+        aq = [keep.tile([P, B], U32, name="aq%d" % c, align_bytes=64) for c in range(4)]
+        asc = [keep.tile([P, B], U8, name="as%d" % c, align_bytes=64) for c in range(4)]
+        wq = [keep.tile([P, H], U32, name="wq%d" % c, align_bytes=64) for c in range(6)]
+        ws = [keep.tile([P, H], U8, name="ws%d" % c, align_bytes=64) for c in range(6)]
+        wbs = [keep.tile([P, B], F32, name="wb%d" % j) for j in range(HT)]
+        hmT = [keep.tile([P, B], F32, name="hmT%d" % j) for j in range(HT)]
+        x1s = [keep.tile([P, H], F32, name="x1_%d" % r) for r in range(RT)]
+        em2 = keep.tile([P, RT], F32, name="em2")
+        em = keep.tile([P, RT], F32, name="em")
+        tiny = keep.tile([P, 1], F32, name="tiny")
+        std = keep.tile([P, RT], F32, name="std")
+        rstd = keep.tile([P, RT], F32, name="rstd")
+        rs = keep.tile([P, RT], F32, name="rs")
+        junk = keep.tile([P, H], BF16, name="junk")
+        raws = {}
+        grps = {}
+        st = {}
+        whole = slice(0, H)
+
+        def half(hf):
+            return slice(512 * hf, 512 * hf + 512)
+
+        def s_col(r):
+            return vec[:, 2 * HT + r:2 * HT + r + 1]
+
+        def t1(key, r, w=1):
+            t = small.tile([P, w], F32, name=key)
+            st[(key, r)] = t
+            return t
+
+        def consts():
+            make_identity(nc, ident[:])
+            nc.vector.memset(vecs_bf[:], 0.0)
+            nc.vector.memset(one1[:], 1.0)
+            nc.vector.memset(brow[:], 0.0)
+            nc.vector.memset(srow[:], 0.0)
+            nc.vector.memset(eps_ln[:], 1e-5)
+            nc.vector.memset(eps_bag[:], 1e-6)
+            nc.vector.memset(tiny[:], 1e-30)
+
+        def small_loads():
+            nc.scalar.dma_start(out=vecs_bf[0:HT, :], in_=b_mb.rearrange("(j p) -> j p", p=P))
+            nc.scalar.dma_start(out=vecs_bf[HT:2 * HT, :], in_=b_b.rearrange("(j p) -> j p", p=P))
+            nc.scalar.dma_start(out=vecs_bf[2 * HT:2 * HT + RT, :], in_=is_bag.rearrange("(r p) a -> r (p a)", p=P))
+            nc.scalar.dma_start(out=brow[0:1, :], in_=ln_b.rearrange("(a n) -> a n", a=1))
+            nc.scalar.dma_start(out=srow[0:1, :], in_=is_bag.rearrange("b a -> a b"))
+            nc.scalar.activation(out=warm[:, 0:1], in_=one1[:], func=ACT.Sqrt)
+
+        def load_rows(dst, src):
+            for r in range(RT):
+                nc.sync.dma_start(out=dst[:, r, :], in_=src[r * P:(r + 1) * P, :])
+
+        def load_chunk(c):
+            w = W_mb if c < 4 else W_b
+            k0 = 512 * (c % 4)
+            raw = rawp.tile([P, 4, H], BF16, name="raw")
+            nc.sync.dma_start(out=raw[:], in_=w[k0:k0 + 512, :].rearrange("(p t) n -> p t n", t=4))
+            raws[c] = raw
+
+        def load_gb():
+            nc.sync.dma_start(out=gb[:, H:2 * H], in_=ln_b.partition_broadcast(P))
+            nc.sync.dma_start(out=gb[:, 0:H], in_=ln_g.partition_broadcast(P))
+
+        def vec_prep():
+            nc.vector.tensor_copy(out=vecs_f[:], in_=vecs_bf[:])
+            vt = bank(4, [P, P], "vt")
+            nc.tensor.transpose(vt[:], vecs_f[:], ident[:])
+            nc.vector.tensor_copy(out=vec[:], in_=vt[:, 0:2 * HT + RT])
+
+        def blend_prep():
+            nc.vector.tensor_copy(out=ident_bf[:], in_=ident[:])
+            for r in PE_BLEND:
+                nc.vector.tensor_scalar(out=dneg[r][:], in0=ident[:], scalar1=s_col(r), scalar2=-1.0, op0=ALU.mult, op1=ALU.mult)
+            nc.vector.tensor_scalar(out=oms[:], in0=vec[:, 2 * HT:2 * HT + RT], scalar1=-1.0, scalar2=1.0, op0=ALU.mult, op1=ALU.add)
+
+        def blend_term_a(r):
+            nc.vector.tensor_scalar(out=q3[:], in0=main_sb[:, r, :], scalar1=oms[:, r:r + 1], scalar2=None, op0=ALU.mult)
+
+        def blend_term_b(r):
+            nc.vector.scalar_tensor_tensor(out=q3[:], in0=b_bc, scalar=s_col(r), in1=q3[:], op0=ALU.mult, op1=ALU.add)
+
+        def turn_act(c, rp):
+            src = main_sb if c < 2 else branch_sb
+            g = c % 2
+            agv = ags[c][:].rearrange("p (b u) -> p b u", u=2)
+            xt = bank((2 * c + rp + 5) % 8, [P, 2, 2, P], "xt")
+            for rr in range(2):
+                words = src[:, 2 * rp + rr, :].bitcast(F32)
+                for u in range(2):
+                    nc.tensor.transpose(xt[:, rr, u, :], words[:, 256 * g + u:256 * g + 256:2], ident[:])
+            nc.scalar.copy(
+                out=agv[:, 256 * rp:256 * rp + 256, :].rearrange("p (rr b) u -> p rr b u", rr=2),
+                in_=xt[:].rearrange("p rr u b -> p rr b u"),
+            )
+
+        def quantise_act(c):
+            nc.vector.quantize_mx(out=aq[c][:].bitcast(FP8X4), scales=asc[c][:], in_=ags[c][:].bitcast(BF16))
+
+        def regroup(c, hh):
+            grp = grpp.tile([P, 512, 4], BF16, name="grp", align_bytes=64)
+            dst = grp[:].rearrange("p (c i) t -> p c t i", i=4)
+            srcv = raws[c][:, :, 512 * hh:512 * hh + 512].rearrange("p t (c i) -> p c t i", i=4)
+            if (c, hh) in SCALAR_UNITS:
+                nc.scalar.copy(out=dst, in_=srcv)
+            else:
+                nc.vector.tensor_copy(out=dst, in_=srcv)
+            grps[(c, hh)] = grp
+
+        def quantise(c, hh):
+            nc.vector.quantize_mx(
+                out=wq[c][:, 512 * hh:512 * hh + 512].bitcast(FP8X4),
+                scales=ws[c][:, 512 * hh:512 * hh + 512],
+                in_=grps[(c, hh)][:].rearrange("p w t -> p (w t)"),
+            )
+
+        def mx(acc, c, j, a, first, last):
+            nc.tensor.matmul_mx(
+                out=acc[:],
+                lhsT=wq[c][:, P * j:P * j + P].bitcast(FP8X4),
+                lhsT_scale=ws[c][:, P * j:P * j + P],
+                rhs=aq[a][:].bitcast(FP8X4),
+                rhs_scale=asc[a][:],
+                start=first,
+                stop=last,
+            )
+
+        def passes1(c, hh):
+            for j in range(4 * hh, 4 * hh + 4):
+                if c == 0:
+                    st[("g1", j)] = bank(j, [P, B], "g1")
+                mx(st[("g1", j)], c, j, c, c == 0, c == 3)
+
+        def gate(j):
+            nc.scalar.activation(out=wbs[j][:], in_=st[("g1", j)][:], func=ACT.Relu, bias=vec[:, j:j + 1])
+
+        def main_norm(r):
+            nc.scalar.activation(out=junk[:], in_=main_sb[:, r, :], func=ACT.Square, accum_out=em2[:, r:r + 1])
+
+        def second_start(j):
+            st[("g2", j)] = bank(j, [P, B], "g2")
+            mx(st[("g2", j)], 4, j, 2, True, False)
+
+        def second_stop(j):
+            mx(st[("g2", j)], 5, j, 3, False, True)
+
+        def product(j, cols):
+            nc.vector.scalar_tensor_tensor(out=hmT[j][:, cols], in0=st[("g2", j)][:, cols], scalar=vec[:, HT + j:HT + j + 1], in1=wbs[j][:, cols], op0=ALU.add, op1=ALU.mult)
+
+        def turn_back(r):
+            hm = [bank(2 * r + hf, [P, 512], "hm") for hf in range(2)]
+            for j in range(HT):
+                nc.tensor.transpose(hm[j // 4][:, P * (j % 4):P * (j % 4) + P], hmT[j][:, P * r:P * r + P], ident[:])
+            st[("hm", r)] = hm
+
+        def n0(r):
+            nc.scalar.activation(out=em[:, r:r + 1], in_=em2[:, r:r + 1], func=ACT.Sqrt, bias=tiny[:])
+
+        def D(r):
+            ssa = t1("ssa", r, 2)
+            for hf in range(2):
+                nc.scalar.activation(out=junk[:, 0:512], in_=st[("hm", r)][hf][:], func=ACT.Square, accum_out=ssa[:, hf:hf + 1])
+
+        def n2(r):
+            ssa = st[("ssa", r)]
+            nc.scalar.activation(out=t1("ss", r)[:], in_=ssa[:, 0:1], func=ACT.Identity, bias=ssa[:, 1:2])
+
+        def sq(r):
+            nc.scalar.activation(out=t1("nrm", r)[:], in_=st[("ss", r)][:], func=ACT.Sqrt, bias=tiny[:])
+            nc.scalar.activation(out=t1("den", r)[:], in_=st[("nrm", r)][:], func=ACT.Identity, bias=eps_bag[:])
+
+        def n4(r):
+            nc.vector.reciprocal(out=t1("rec", r)[:], in_=st[("den", r)][:])
+
+        def n5(r):
+            nc.vector.tensor_scalar(out=t1("alpha", r)[:], in0=st[("rec", r)][:], scalar1=em[:, r:r + 1], scalar2=1.0, op0=ALU.mult, op1=ALU.min)
+
+        def F(r, hf):
+            if hf == 0:
+                st[("pre", r)] = work.tile([P, H], F32, name="pre", bufs=3)
+                t1("sp", r, 2)
+            nc.vector.scalar_tensor_tensor(out=st[("pre", r)][:, half(hf)], in0=st[("hm", r)][hf][:], scalar=st[("alpha", r)][:], in1=main_sb[:, r, half(hf)], op0=ALU.mult, op1=ALU.add, accum_out=st[("sp", r)][:, hf:hf + 1])
+
+        def nm(r):
+            sp = st[("sp", r)]
+            nc.vector.tensor_scalar(out=t1("negmu", r)[:], in0=sp[:, 0:1], scalar1=sp[:, 1:2], scalar2=-1.0 / H, op0=ALU.add, op1=ALU.mult)
+
+        def Var(r):
+            nc.scalar.activation(out=junk[:], in_=st[("pre", r)][:], func=ACT.Square, bias=st[("negmu", r)][:], accum_out=t1("vs", r)[:])
+            nc.scalar.activation(out=std[:, r:r + 1], in_=st[("vs", r)][:], func=ACT.Sqrt, scale=1.0 / H, bias=eps_ln[:])
+
+        def rA(r):
+            nc.vector.reciprocal(out=rstd[:, r:r + 1], in_=std[:, r:r + 1])
+
+        def rB(r):
+            nc.vector.tensor_tensor(out=rs[:, r:r + 1], in0=rstd[:, r:r + 1], in1=s_col(r), op=ALU.mult)
+
+        def I(r, hf):
+            nc.vector.scalar_tensor_tensor(out=x1s[r][:, half(hf)], in0=st[("pre", r)][:, half(hf)], scalar=st[("negmu", r)][:], in1=g_bc[:, half(hf)], op0=ALU.add, op1=ALU.mult)
+
+        def R(r):
+            rb = [bank(2 * r + hf, [P, 512], "rb") for hf in range(2)]
+            for hf in range(2):
+                nc.tensor.matmul(out=rb[hf][:], lhsT=ident_bf[:], rhs=main_sb[:, r, half(hf)], start=True, stop=False)
+                nc.tensor.matmul(out=rb[hf][:], lhsT=dneg[r][:], rhs=main_sb[:, r, half(hf)], start=False, stop=False)
+                nc.tensor.matmul(out=rb[hf][:], lhsT=srow[:, P * r:P * r + P], rhs=brow[:, half(hf)], start=False, stop=True)
+            st[("rb", r)] = rb
+
+        def K(r, hf):
+            st[("sc", r)] = x1s[r]
+            q = st[("rb", r)][hf][:] if r in PE_BLEND else q3[:, half(hf)]
+            nc.vector.scalar_tensor_tensor(out=st[("sc", r)][:, half(hf)], in0=x1s[r][:, half(hf)], scalar=rs[:, r:r + 1], in1=q, op0=ALU.mult, op1=ALU.add)
+
+        def store(dst, key, r, cols):
+            nc.sync.dma_start(out=dst[r * P:(r + 1) * P, cols], in_=st[(key, r)][:, cols])
+
+        def tanh_table():
+            nc.scalar.activation(out=warm[:, 1:2], in_=one1[:], func=ACT.Tanh)
+
+        def L(r, cols):
+            if ("th", r) not in st:
+                st[("th", r)] = work.tile([P, H], F32, name="th", bufs=4)
+            nc.scalar.activation(out=st[("th", r)][:, cols], in_=st[("sc", r)][:, cols], func=ACT.Tanh)
+
+        def M(r, cols, eng):
+            eng.tensor_tensor(out=st[("th", r)][:, cols], in0=st[("th", r)][:, cols], in1=o_sb[:, r, cols], op=ALU.mult)
+            store(out_0, "th", r, cols)
+
+        consts()
+        small_loads()
+        load_chunk(0)
+        load_rows(main_sb, main)
+        load_chunk(1)
+        load_rows(branch_sb, branch)
+        load_chunk(2)
+        load_chunk(3)
+        vec_prep()
+        regroup(0, 0)
+        regroup(0, 1)
+        load_chunk(4)
+        blend_prep()
+        quantise(0, 0)
+        for c in range(2):
+            for rp in range(2):
+                turn_act(c, rp)
+        quantise(0, 1)
+        quantise_act(0)
+        quantise_act(1)
+        regroup(1, 0)
+        regroup(1, 1)
+        load_chunk(5)
+        load_gb()
+        load_rows(o_sb, o)
+        blend_term_a(3)
+        quantise(1, 0)
+        for c in range(2, 4):
+            for rp in range(2):
+                turn_act(c, rp)
+        passes1(0, 0)
+        passes1(0, 1)
+        passes1(1, 0)
+        quantise(1, 1)
+        passes1(1, 1)
+        quantise_act(2)
+        for c in range(2, 4):
+            regroup(c, 0)
+            regroup(c, 1)
+            if c == 2:
+                quantise_act(3)
+            if c == 3:
+                quantise(2, 1)
+                passes1(2, 1)
+            quantise(c, 0)
+            passes1(c, 0)
+        main_norm(0)
+        regroup(4, 0)
+        quantise(3, 1)
+        passes1(3, 1)
+        for j in range(4):
+            gate(j)
+        regroup(4, 1)
+        quantise(4, 0)
+        for j in range(4):
+            second_start(j)
+        regroup(5, 0)
+        regroup(5, 1)
+        for j in range(4, HT):
+            gate(j)
+        quantise(4, 1)
+        quantise(5, 0)
+        for j in range(4):
+            second_stop(j)
+        quantise(5, 1)
+        for j in range(4, HT):
+            second_start(j)
+            second_stop(j)
+        n0(0)
+        main_norm(1)
+        n0(1)
+        for j in range(4):
+            product(j, slice(0, B))
+        for j in range(4, HT):
+            product(j, slice(0, P))
+        for j in range(4, HT):
+            product(j, slice(P, B))
+        blend_term_b(3)
+        for r in range(RT):
+            turn_back(r)
+        D(0); n2(0); sq(0); n4(0); n5(0)
+        D(1)
+        main_norm(2)
+        n0(2)
+        for r in range(RT):
+            nx = r + 1
+            F(r, 0)
+            if r > 0:
+                rA(r - 1)
+            F(r, 1)
+            if r in PE_BLEND:
+                R(r)
+            if r > 0:
+                rB(r - 1)
+            if nx < RT:
+                n2(nx)
+                sq(nx)
+            nm(r)
+            Var(r)
+            if nx + 1 < RT:
+                D(nx + 1)
+            if r == 1:
+                main_norm(3)
+                n0(3)
+            if r > 0:
+                K(r - 1, 0)
+            if nx < RT:
+                n4(nx)
+            I(r, 0)
+            if nx < RT:
+                n5(nx)
+            if r > 0:
+                K(r - 1, 1)
+                store(out_1, "sc", r - 1, whole)
+            I(r, 1)
+        tanh_table()
+        for r in range(RT - 1):
+            L(r, whole)
+        rA(RT - 1)
+        rB(RT - 1)
+        for hf in range(2):
+            K(RT - 1, hf)
+            store(out_1, "sc", RT - 1, half(hf))
+            L(RT - 1, half(hf))
+        for r in range(RT - 1):
+            M(r, whole, nc.vector)
+        for hf in range(2):
+            M(RT - 1, half(hf), nc.vector)

@@ -121,7 +121,7 @@ def tile_bag_lstm_pb_kernel(tc, main, branch, o, is_bag, W_mb, b_mb, W_b, b_b, l
 
         def vec_prep():
             nc.vector.tensor_copy(out=vecs_f[:], in_=vecs_bf[:])
-            vt = bank(4, [P, P], "vt")
+            vt = bank(3, [P, P], "vt")
             nc.tensor.transpose(vt[:], vecs_f[:], ident[:])
             nc.vector.tensor_copy(out=vec[:], in_=vt[:, 0:2 * HT + RT])
 
@@ -141,7 +141,7 @@ def tile_bag_lstm_pb_kernel(tc, main, branch, o, is_bag, W_mb, b_mb, W_b, b_b, l
             src = main_sb if c < 2 else branch_sb
             g = c % 2
             agv = ags[c][:].rearrange("p (b u) -> p b u", u=2)
-            xt = bank((2 * c + rp + 5) % 8, [P, 2, 2, P], "xt")
+            xt = bank(4 + (2 * c + rp) % 4, [P, 2, 2, P], "xt")
             for rr in range(2):
                 words = src[:, 2 * rp + rr, :].bitcast(F32)
                 for u in range(2):
@@ -310,10 +310,10 @@ def tile_bag_lstm_pb_kernel(tc, main, branch, o, is_bag, W_mb, b_mb, W_b, b_b, l
         load_rows(o_sb, o)
         blend_term_a(3)
         quantise(1, 0)
+        passes1(0, 0)
         for c in range(2, 4):
             for rp in range(2):
                 turn_act(c, rp)
-        passes1(0, 0)
         passes1(0, 1)
         passes1(1, 0)
         quantise(1, 1)

@@ -17,7 +17,7 @@ H = 1024
 RT = B // P
 HT = H // P
 FLOPS = 2 * B * (2 * H) * H + 2 * B * H * H
-SCALAR_UNITS = ((0, 1), (1, 1), (2, 1), (3, 1), (5, 1))
+SCALAR_UNITS = ((0, 1), (2, 1), (3, 1), (4, 1))
 PE_BLEND = (0, 1, 2)
 
 
@@ -67,6 +67,7 @@ def tile_bag_lstm_pb_kernel(tc, main, branch, o, is_bag, W_mb, b_mb, W_b, b_b, l
         em = keep.tile([P, RT], F32, name="em")
         tiny = keep.tile([P, 1], F32, name="tiny")
         std = keep.tile([P, RT], F32, name="std")
+        vs = keep.tile([P, RT], F32, name="vs")
         rstd = keep.tile([P, RT], F32, name="rstd")
         rs = keep.tile([P, RT], F32, name="rs")
         junk = keep.tile([P, H], BF16, name="junk")
@@ -119,11 +120,15 @@ def tile_bag_lstm_pb_kernel(tc, main, branch, o, is_bag, W_mb, b_mb, W_b, b_b, l
             nc.sync.dma_start(out=gb[:, H:2 * H], in_=ln_b.partition_broadcast(P))
             nc.sync.dma_start(out=gb[:, 0:H], in_=ln_g.partition_broadcast(P))
 
-        def vec_prep():
+        def vec_cast():
             nc.vector.tensor_copy(out=vecs_f[:], in_=vecs_bf[:])
-            vt = bank(3, [P, P], "vt")
-            nc.tensor.transpose(vt[:], vecs_f[:], ident[:])
-            nc.vector.tensor_copy(out=vec[:], in_=vt[:, 0:2 * HT + RT])
+
+        def vec_turn():
+            st["vt"] = bank(3, [P, P], "vt")
+            nc.tensor.transpose(st["vt"][:], vecs_f[:], ident[:])
+
+        def vec_copy():
+            nc.vector.tensor_copy(out=vec[:], in_=st["vt"][:, 0:2 * HT + RT])
 
         def blend_prep():
             nc.vector.tensor_copy(out=ident_bf[:], in_=ident[:])
@@ -137,7 +142,7 @@ def tile_bag_lstm_pb_kernel(tc, main, branch, o, is_bag, W_mb, b_mb, W_b, b_b, l
         def blend_term_b(r):
             nc.vector.scalar_tensor_tensor(out=q3[:], in0=b_bc, scalar=s_col(r), in1=q3[:], op0=ALU.mult, op1=ALU.add)
 
-        def turn_act(c, rp):
+        def turn_act(c, rp, copy=nc.scalar.copy):
             src = main_sb if c < 2 else branch_sb
             g = c % 2
             agv = ags[c][:].rearrange("p (b u) -> p b u", u=2)
@@ -146,7 +151,7 @@ def tile_bag_lstm_pb_kernel(tc, main, branch, o, is_bag, W_mb, b_mb, W_b, b_b, l
                 words = src[:, 2 * rp + rr, :].bitcast(F32)
                 for u in range(2):
                     nc.tensor.transpose(xt[:, rr, u, :], words[:, 256 * g + u:256 * g + 256:2], ident[:])
-            nc.scalar.copy(
+            copy(
                 out=agv[:, 256 * rp:256 * rp + 256, :].rearrange("p (rr b) u -> p rr b u", rr=2),
                 in_=xt[:].rearrange("p rr u b -> p rr b u"),
             )
@@ -210,20 +215,17 @@ def tile_bag_lstm_pb_kernel(tc, main, branch, o, is_bag, W_mb, b_mb, W_b, b_b, l
                 nc.tensor.transpose(hm[j // 4][:, P * (j % 4):P * (j % 4) + P], hmT[j][:, P * r:P * r + P], ident[:])
             st[("hm", r)] = hm
 
-        def n0(r):
-            nc.scalar.activation(out=em[:, r:r + 1], in_=em2[:, r:r + 1], func=ACT.Sqrt, bias=tiny[:])
+        def n0():
+            nc.scalar.activation(out=em[:], in_=em2[:], func=ACT.Sqrt)
 
         def D(r):
             ssa = t1("ssa", r, 2)
             for hf in range(2):
                 nc.scalar.activation(out=junk[:, 0:512], in_=st[("hm", r)][hf][:], func=ACT.Square, accum_out=ssa[:, hf:hf + 1])
 
-        def n2(r):
-            ssa = st[("ssa", r)]
-            nc.scalar.activation(out=t1("ss", r)[:], in_=ssa[:, 0:1], func=ACT.Identity, bias=ssa[:, 1:2])
-
         def sq(r):
-            nc.scalar.activation(out=t1("nrm", r)[:], in_=st[("ss", r)][:], func=ACT.Sqrt, bias=tiny[:])
+            ssa = st[("ssa", r)]
+            nc.scalar.activation(out=t1("nrm", r)[:], in_=ssa[:, 0:1], func=ACT.Sqrt, bias=ssa[:, 1:2])
             nc.scalar.activation(out=t1("den", r)[:], in_=st[("nrm", r)][:], func=ACT.Identity, bias=eps_bag[:])
 
         def n4(r):
@@ -234,7 +236,7 @@ def tile_bag_lstm_pb_kernel(tc, main, branch, o, is_bag, W_mb, b_mb, W_b, b_b, l
 
         def F(r, hf):
             if hf == 0:
-                st[("pre", r)] = work.tile([P, H], F32, name="pre", bufs=3)
+                st[("pre", r)] = work.tile([P, H], F32, name="pre", bufs=4)
                 t1("sp", r, 2)
             nc.vector.scalar_tensor_tensor(out=st[("pre", r)][:, half(hf)], in0=st[("hm", r)][hf][:], scalar=st[("alpha", r)][:], in1=main_sb[:, r, half(hf)], op0=ALU.mult, op1=ALU.add, accum_out=st[("sp", r)][:, hf:hf + 1])
 
@@ -243,17 +245,19 @@ def tile_bag_lstm_pb_kernel(tc, main, branch, o, is_bag, W_mb, b_mb, W_b, b_b, l
             nc.vector.tensor_scalar(out=t1("negmu", r)[:], in0=sp[:, 0:1], scalar1=sp[:, 1:2], scalar2=-1.0 / H, op0=ALU.add, op1=ALU.mult)
 
         def Var(r):
-            nc.scalar.activation(out=junk[:], in_=st[("pre", r)][:], func=ACT.Square, bias=st[("negmu", r)][:], accum_out=t1("vs", r)[:])
-            nc.scalar.activation(out=std[:, r:r + 1], in_=st[("vs", r)][:], func=ACT.Sqrt, scale=1.0 / H, bias=eps_ln[:])
+            nc.scalar.activation(out=junk[:], in_=st[("pre", r)][:], func=ACT.Square, bias=st[("negmu", r)][:], accum_out=vs[:, r:r + 1])
 
-        def rA(r):
-            nc.vector.reciprocal(out=rstd[:, r:r + 1], in_=std[:, r:r + 1])
+        def deviation(r, n):
+            nc.scalar.activation(out=std[:, r:r + n], in_=vs[:, r:r + n], func=ACT.Sqrt, scale=1.0 / H, bias=eps_ln[:])
 
-        def rB(r):
-            nc.vector.tensor_tensor(out=rs[:, r:r + 1], in0=rstd[:, r:r + 1], in1=s_col(r), op=ALU.mult)
+        def rA(r, n):
+            nc.vector.reciprocal(out=rstd[:, r:r + n], in_=std[:, r:r + n])
 
-        def I(r, hf):
-            nc.vector.scalar_tensor_tensor(out=x1s[r][:, half(hf)], in0=st[("pre", r)][:, half(hf)], scalar=st[("negmu", r)][:], in1=g_bc[:, half(hf)], op0=ALU.add, op1=ALU.mult)
+        def rB(r, n):
+            nc.vector.tensor_tensor(out=rs[:, r:r + n], in0=rstd[:, r:r + n], in1=vec[:, 2 * HT + r:2 * HT + r + n], op=ALU.mult)
+
+        def I(r):
+            nc.vector.scalar_tensor_tensor(out=x1s[r][:], in0=st[("pre", r)][:], scalar=st[("negmu", r)][:], in1=g_bc, op0=ALU.add, op1=ALU.mult)
 
         def R(r):
             rb = [bank(2 * r + hf, [P, 512], "rb") for hf in range(2)]
@@ -291,7 +295,9 @@ def tile_bag_lstm_pb_kernel(tc, main, branch, o, is_bag, W_mb, b_mb, W_b, b_b, l
         load_rows(branch_sb, branch)
         load_chunk(2)
         load_chunk(3)
-        vec_prep()
+        vec_cast()
+        vec_turn()
+        vec_copy()
         regroup(0, 0)
         regroup(0, 1)
         load_chunk(4)
@@ -301,14 +307,16 @@ def tile_bag_lstm_pb_kernel(tc, main, branch, o, is_bag, W_mb, b_mb, W_b, b_b, l
             for rp in range(2):
                 turn_act(c, rp)
         quantise(0, 1)
+        blend_term_a(3)
         quantise_act(0)
-        quantise_act(1)
         regroup(1, 0)
+        quantise_act(1)
+        main_norm(0)
+        main_norm(1)
         regroup(1, 1)
         load_chunk(5)
         load_gb()
         load_rows(o_sb, o)
-        blend_term_a(3)
         quantise(1, 0)
         passes1(0, 0)
         for c in range(2, 4):
@@ -318,32 +326,30 @@ def tile_bag_lstm_pb_kernel(tc, main, branch, o, is_bag, W_mb, b_mb, W_b, b_b, l
         passes1(1, 0)
         quantise(1, 1)
         passes1(1, 1)
+        regroup(2, 0)
         quantise_act(2)
-        for c in range(2, 4):
-            regroup(c, 0)
-            regroup(c, 1)
-            if c == 2:
-                quantise_act(3)
-            if c == 3:
-                quantise(2, 1)
-                passes1(2, 1)
-            quantise(c, 0)
-            passes1(c, 0)
-        main_norm(0)
+        regroup(2, 1)
+        quantise(2, 0)
+        quantise_act(3)
+        passes1(2, 0)
+        regroup(3, 0)
+        regroup(3, 1)
+        quantise(2, 1)
+        passes1(2, 1)
+        quantise(3, 0)
+        passes1(3, 0)
         regroup(4, 0)
+        regroup(4, 1)
         quantise(3, 1)
         passes1(3, 1)
-        for j in range(4):
+        for j in range(HT):
             gate(j)
-        regroup(4, 1)
         quantise(4, 0)
+        regroup(5, 0)
+        quantise(4, 1)
         for j in range(4):
             second_start(j)
-        regroup(5, 0)
         regroup(5, 1)
-        for j in range(4, HT):
-            gate(j)
-        quantise(4, 1)
         quantise(5, 0)
         for j in range(4):
             second_stop(j)
@@ -351,9 +357,9 @@ def tile_bag_lstm_pb_kernel(tc, main, branch, o, is_bag, W_mb, b_mb, W_b, b_b, l
         for j in range(4, HT):
             second_start(j)
             second_stop(j)
-        n0(0)
-        main_norm(1)
-        n0(1)
+        for r in range(2, RT):
+            main_norm(r)
+        n0()
         for j in range(4):
             product(j, slice(0, B))
         for j in range(4, HT):
@@ -363,50 +369,52 @@ def tile_bag_lstm_pb_kernel(tc, main, branch, o, is_bag, W_mb, b_mb, W_b, b_b, l
         blend_term_b(3)
         for r in range(RT):
             turn_back(r)
-        D(0); n2(0); sq(0); n4(0); n5(0)
+        D(0)
+        sq(0)
+        n4(0)
+        n5(0)
         D(1)
-        main_norm(2)
-        n0(2)
+        sq(1)
         for r in range(RT):
-            nx = r + 1
             F(r, 0)
             if r > 0:
-                rA(r - 1)
+                nm(r - 1)
+            if r + 1 < RT:
+                n4(r + 1)
             F(r, 1)
+            if r + 1 < RT:
+                n5(r + 1)
             if r in PE_BLEND:
                 R(r)
+            if r + 2 < RT:
+                D(r + 2)
+                sq(r + 2)
             if r > 0:
-                rB(r - 1)
-            if nx < RT:
-                n2(nx)
-                sq(nx)
-            nm(r)
-            Var(r)
-            if nx + 1 < RT:
-                D(nx + 1)
-            if r == 1:
-                main_norm(3)
-                n0(3)
-            if r > 0:
-                K(r - 1, 0)
-            if nx < RT:
-                n4(nx)
-            I(r, 0)
-            if nx < RT:
-                n5(nx)
-            if r > 0:
-                K(r - 1, 1)
-                store(out_1, "sc", r - 1, whole)
-            I(r, 1)
+                Var(r - 1)
+        deviation(0, 2)
+        nm(RT - 1)
+        I(0)
+        rA(0, 2)
+        Var(RT - 1)
+        deviation(2, 2)
         tanh_table()
-        for r in range(RT - 1):
-            L(r, whole)
-        rA(RT - 1)
-        rB(RT - 1)
-        for hf in range(2):
-            K(RT - 1, hf)
-            store(out_1, "sc", RT - 1, half(hf))
-            L(RT - 1, half(hf))
+        I(1)
+        rB(0, 2)
+        for r in range(RT):
+            for hf in range(2):
+                K(r, hf)
+                if r == RT - 1:
+                    store(out_1, "sc", r, half(hf))
+                    L(r, half(hf))
+            if r < RT - 1:
+                store(out_1, "sc", r, whole)
+                L(r, whole)
+            if r == 0:
+                rA(2, 2)
+            if r + 2 < RT:
+                I(r + 2)
+            if r == 0:
+                rB(2, 2)
         for r in range(RT - 1):
             M(r, whole, nc.vector)
         for hf in range(2):

@@ -161,8 +161,8 @@ def tile_bag_lstm_pb_kernel(tc, main, branch, o, is_bag, W_mb, b_mb, W_b, b_b, l
 
         def regroup(c, hh):
             grp = grpp.tile([P, 512, 4], BF16, name="grp", align_bytes=64)
-            dst = grp[:].rearrange("p (c i) t -> p c t i", i=4)
-            srcv = raws[c][:, :, 512 * hh:512 * hh + 512].rearrange("p t (c i) -> p c t i", i=4)
+            dst = grp[:].rearrange("p (c i) t -> p c t i", i=8)
+            srcv = raws[c][:, :, 512 * hh:512 * hh + 512].rearrange("p t (c i) -> p c t i", i=8)
             if (c, hh) in SCALAR_UNITS:
                 nc.scalar.copy(out=dst, in_=srcv)
             else:

@@ -18,7 +18,7 @@ RT = B // P
 HT = H // P
 FLOPS = 2 * B * (2 * H) * H + 2 * B * H * H
 SCALAR_UNITS = ((0, 1), (2, 1), (3, 1), (4, 1))
-PE_BLEND = (0, 1, 2)
+PE_BLEND = (1, 2, 3)
 
 
 def tile_bag_lstm_pb_kernel(tc, main, branch, o, is_bag, W_mb, b_mb, W_b, b_b, ln_g, ln_b, out_0, out_1):
@@ -27,19 +27,22 @@ def tile_bag_lstm_pb_kernel(tc, main, branch, o, is_bag, W_mb, b_mb, W_b, b_b, l
         keep = ctx.enter_context(tc.tile_pool(name="keep", bufs=1))
         rawp = ctx.enter_context(tc.tile_pool(name="rawp", bufs=4))
         grpp = ctx.enter_context(tc.tile_pool(name="grpp", bufs=4))
-        work = ctx.enter_context(tc.tile_pool(name="work", bufs=2))
+        work = ctx.enter_context(tc.tile_pool(name="work", bufs=4))
         small = ctx.enter_context(tc.tile_pool(name="small", bufs=4))
         psum = ctx.enter_context(tc.psum_pool(name="psum", bufs=1))
         ctx.enter_context(tc.manual_schedule())
 
-        def bank(i, shape, name):
-            return psum.tile(shape, F32, tag="bank%d" % i, name=name)
+        def bank(i, shape, name, dtype=F32):
+            return psum.tile(shape, dtype, tag="bank%d" % i, name=name)
 
         ident = keep.tile([P, P], F32, name="ident")
         ident_bf = keep.tile([P, P], BF16, name="ident_bf")
         vecs_bf = keep.tile([P, P], BF16, name="vecs_bf")
         vecs_f = keep.tile([P, P], F32, name="vecs_f")
-        vec = keep.tile([P, 2 * HT + RT], F32, name="vec")
+        vec = keep.tile([P, 3 * HT], F32, name="vec")
+        gain_col = keep.tile([P, HT], BF16, name="gain_col")
+        s_bf = keep.tile([P, RT], BF16, name="s_bf")
+        s_f = keep.tile([P, RT], F32, name="s_f")
         one1 = keep.tile([P, 1], F32, name="one1")
         eps_ln = keep.tile([P, 1], F32, name="eps_ln")
         eps_bag = keep.tile([P, 1], F32, name="eps_bag")
@@ -50,11 +53,9 @@ def tile_bag_lstm_pb_kernel(tc, main, branch, o, is_bag, W_mb, b_mb, W_b, b_b, l
         main_sb = keep.tile([P, RT, H], BF16, name="main_sb")
         branch_sb = keep.tile([P, RT, H], BF16, name="branch_sb")
         o_sb = keep.tile([P, RT, H], BF16, name="o_sb")
-        gb = keep.tile([P, 2 * H], BF16, name="gb")
-        g_bc = gb[:, 0:H]
-        b_bc = gb[:, H:2 * H]
-        q3 = keep.tile([P, H], F32, name="q3")
-        dneg = [keep.tile([P, P], BF16, name="dneg%d" % r) for r in PE_BLEND]
+        b_bc = keep.tile([P, H], BF16, name="b_bc")
+        q0 = keep.tile([P, H], F32, name="q0")
+        dneg = {r: keep.tile([P, P], BF16, name="dneg%d" % r) for r in PE_BLEND}
         ags = [keep.tile([P, 2 * B], F32, name="ag%d" % c, align_bytes=64) for c in range(4)]
         aq = [keep.tile([P, B], U32, name="aq%d" % c, align_bytes=64) for c in range(4)]
         asc = [keep.tile([P, B], U8, name="as%d" % c, align_bytes=64) for c in range(4)]
@@ -65,11 +66,11 @@ def tile_bag_lstm_pb_kernel(tc, main, branch, o, is_bag, W_mb, b_mb, W_b, b_b, l
         x1s = [keep.tile([P, H], F32, name="x1_%d" % r) for r in range(RT)]
         em2 = keep.tile([P, RT], F32, name="em2")
         em = keep.tile([P, RT], F32, name="em")
-        tiny = keep.tile([P, 1], F32, name="tiny")
-        std = keep.tile([P, RT], F32, name="std")
         vs = keep.tile([P, RT], F32, name="vs")
-        rstd = keep.tile([P, RT], F32, name="rstd")
-        rs = keep.tile([P, RT], F32, name="rs")
+        inv_root = keep.tile([P, 2], F32, name="inv_root")
+        var_g = keep.tile([P, 2], F32, name="var_g")
+        rstd_g = keep.tile([P, 2], F32, name="rstd_g")
+        rs_g = keep.tile([P, 2], F32, name="rs_g")
         junk = keep.tile([P, H], BF16, name="junk")
         raws = {}
         grps = {}
@@ -80,7 +81,7 @@ def tile_bag_lstm_pb_kernel(tc, main, branch, o, is_bag, W_mb, b_mb, W_b, b_b, l
             return slice(512 * hf, 512 * hf + 512)
 
         def s_col(r):
-            return vec[:, 2 * HT + r:2 * HT + r + 1]
+            return s_f[:, r:r + 1]
 
         def t1(key, r, w=1):
             t = small.tile([P, w], F32, name=key)
@@ -95,19 +96,20 @@ def tile_bag_lstm_pb_kernel(tc, main, branch, o, is_bag, W_mb, b_mb, W_b, b_b, l
             nc.vector.memset(srow[:], 0.0)
             nc.vector.memset(eps_ln[:], 1e-5)
             nc.vector.memset(eps_bag[:], 1e-6)
-            nc.vector.memset(tiny[:], 1e-30)
+            nc.gpsimd.memset(inv_root[:], -0.5)
 
         def small_loads():
-            nc.scalar.dma_start(out=vecs_bf[0:HT, :], in_=b_mb.rearrange("(j p) -> j p", p=P))
-            nc.scalar.dma_start(out=vecs_bf[HT:2 * HT, :], in_=b_b.rearrange("(j p) -> j p", p=P))
-            nc.scalar.dma_start(out=vecs_bf[2 * HT:2 * HT + RT, :], in_=is_bag.rearrange("(r p) a -> r (p a)", p=P))
+            for i, src in enumerate((b_mb, b_b, ln_g)):
+                nc.scalar.dma_start(out=vecs_bf[HT * i:HT * i + HT, :], in_=src.rearrange("(j p) -> j p", p=P))
+            nc.scalar.dma_start(out=s_bf[:], in_=is_bag.rearrange("(p r) a -> p (r a)", r=RT))
             nc.scalar.dma_start(out=brow[0:1, :], in_=ln_b.rearrange("(a n) -> a n", a=1))
             nc.scalar.dma_start(out=srow[0:1, :], in_=is_bag.rearrange("b a -> a b"))
             nc.scalar.activation(out=warm[:, 0:1], in_=one1[:], func=ACT.Sqrt)
 
         def load_rows(dst, src):
-            for r in range(RT):
-                nc.sync.dma_start(out=dst[:, r, :], in_=src[r * P:(r + 1) * P, :])
+            rows = src.rearrange("(p r) n -> p r n", r=RT)
+            for r in range(0, RT, 2):
+                nc.sync.dma_start(out=dst[:, r:r + 2, :], in_=rows[:, r:r + 2, :])
 
         def load_chunk(c):
             w = W_mb if c < 4 else W_b
@@ -116,9 +118,8 @@ def tile_bag_lstm_pb_kernel(tc, main, branch, o, is_bag, W_mb, b_mb, W_b, b_b, l
             nc.sync.dma_start(out=raw[:], in_=w[k0:k0 + 512, :].rearrange("(p t) n -> p t n", t=4))
             raws[c] = raw
 
-        def load_gb():
-            nc.sync.dma_start(out=gb[:, H:2 * H], in_=ln_b.partition_broadcast(P))
-            nc.sync.dma_start(out=gb[:, 0:H], in_=ln_g.partition_broadcast(P))
+        def load_bias():
+            nc.sync.dma_start(out=b_bc[:], in_=ln_b.partition_broadcast(P))
 
         def vec_cast():
             nc.vector.tensor_copy(out=vecs_f[:], in_=vecs_bf[:])
@@ -128,21 +129,21 @@ def tile_bag_lstm_pb_kernel(tc, main, branch, o, is_bag, W_mb, b_mb, W_b, b_b, l
             nc.tensor.transpose(st["vt"][:], vecs_f[:], ident[:])
 
         def vec_copy():
-            nc.vector.tensor_copy(out=vec[:], in_=st["vt"][:, 0:2 * HT + RT])
-
-        def blend_prep():
+            nc.vector.tensor_copy(out=s_f[:], in_=s_bf[:])
+            nc.vector.tensor_copy(out=vec[:], in_=st["vt"][:, 0:3 * HT])
             nc.vector.tensor_copy(out=ident_bf[:], in_=ident[:])
+            nc.vector.tensor_scalar(out=oms[:], in0=s_f[:], scalar1=-1.0, scalar2=1.0, op0=ALU.mult, op1=ALU.add)
+            nc.vector.tensor_copy(out=gain_col[:], in_=vec[:, 2 * HT:3 * HT])
             for r in PE_BLEND:
                 nc.vector.tensor_scalar(out=dneg[r][:], in0=ident[:], scalar1=s_col(r), scalar2=-1.0, op0=ALU.mult, op1=ALU.mult)
-            nc.vector.tensor_scalar(out=oms[:], in0=vec[:, 2 * HT:2 * HT + RT], scalar1=-1.0, scalar2=1.0, op0=ALU.mult, op1=ALU.add)
 
-        def blend_term_a(r):
-            nc.vector.tensor_scalar(out=q3[:], in0=main_sb[:, r, :], scalar1=oms[:, r:r + 1], scalar2=None, op0=ALU.mult)
+        def blend_term_a():
+            nc.vector.tensor_scalar(out=q0[:], in0=main_sb[:, 0, :], scalar1=oms[:, 0:1], scalar2=None, op0=ALU.mult)
 
-        def blend_term_b(r):
-            nc.vector.scalar_tensor_tensor(out=q3[:], in0=b_bc, scalar=s_col(r), in1=q3[:], op0=ALU.mult, op1=ALU.add)
+        def blend_term_b():
+            nc.vector.scalar_tensor_tensor(out=q0[:], in0=b_bc[:], scalar=s_col(0), in1=q0[:], op0=ALU.mult, op1=ALU.add)
 
-        def turn_act(c, rp, copy=nc.scalar.copy):
+        def turn_act(c, rp):
             src = main_sb if c < 2 else branch_sb
             g = c % 2
             agv = ags[c][:].rearrange("p (b u) -> p b u", u=2)
@@ -151,7 +152,7 @@ def tile_bag_lstm_pb_kernel(tc, main, branch, o, is_bag, W_mb, b_mb, W_b, b_b, l
                 words = src[:, 2 * rp + rr, :].bitcast(F32)
                 for u in range(2):
                     nc.tensor.transpose(xt[:, rr, u, :], words[:, 256 * g + u:256 * g + 256:2], ident[:])
-            copy(
+            nc.scalar.copy(
                 out=agv[:, 256 * rp:256 * rp + 256, :].rearrange("p (rr b) u -> p rr b u", rr=2),
                 in_=xt[:].rearrange("p rr u b -> p rr b u"),
             )
@@ -199,6 +200,9 @@ def tile_bag_lstm_pb_kernel(tc, main, branch, o, is_bag, W_mb, b_mb, W_b, b_b, l
         def main_norm(r):
             nc.scalar.activation(out=junk[:], in_=main_sb[:, r, :], func=ACT.Square, accum_out=em2[:, r:r + 1])
 
+        def main_root():
+            nc.scalar.activation(out=em[:], in_=em2[:], func=ACT.Sqrt)
+
         def second_start(j):
             st[("g2", j)] = bank(j, [P, B], "g2")
             mx(st[("g2", j)], 4, j, 2, True, False)
@@ -215,77 +219,85 @@ def tile_bag_lstm_pb_kernel(tc, main, branch, o, is_bag, W_mb, b_mb, W_b, b_b, l
                 nc.tensor.transpose(hm[j // 4][:, P * (j % 4):P * (j % 4) + P], hmT[j][:, P * r:P * r + P], ident[:])
             st[("hm", r)] = hm
 
-        def n0():
-            nc.scalar.activation(out=em[:], in_=em2[:], func=ACT.Sqrt)
-
         def D(r):
             ssa = t1("ssa", r, 2)
             for hf in range(2):
                 nc.scalar.activation(out=junk[:, 0:512], in_=st[("hm", r)][hf][:], func=ACT.Square, accum_out=ssa[:, hf:hf + 1])
 
-        def sq(r):
+        def norm(r):
             ssa = st[("ssa", r)]
             nc.scalar.activation(out=t1("nrm", r)[:], in_=ssa[:, 0:1], func=ACT.Sqrt, bias=ssa[:, 1:2])
             nc.scalar.activation(out=t1("den", r)[:], in_=st[("nrm", r)][:], func=ACT.Identity, bias=eps_bag[:])
 
-        def n4(r):
+        def alpha_a(r):
             nc.vector.reciprocal(out=t1("rec", r)[:], in_=st[("den", r)][:])
 
-        def n5(r):
+        def alpha_b(r):
             nc.vector.tensor_scalar(out=t1("alpha", r)[:], in0=st[("rec", r)][:], scalar1=em[:, r:r + 1], scalar2=1.0, op0=ALU.mult, op1=ALU.min)
 
         def F(r, hf):
             if hf == 0:
-                st[("pre", r)] = work.tile([P, H], F32, name="pre", bufs=4)
+                st[("pre", r)] = work.tile([P, H], F32, name="pre")
                 t1("sp", r, 2)
             nc.vector.scalar_tensor_tensor(out=st[("pre", r)][:, half(hf)], in0=st[("hm", r)][hf][:], scalar=st[("alpha", r)][:], in1=main_sb[:, r, half(hf)], op0=ALU.mult, op1=ALU.add, accum_out=st[("sp", r)][:, hf:hf + 1])
 
-        def nm(r):
+        def mean(r):
             sp = st[("sp", r)]
-            nc.vector.tensor_scalar(out=t1("negmu", r)[:], in0=sp[:, 0:1], scalar1=sp[:, 1:2], scalar2=-1.0 / H, op0=ALU.add, op1=ALU.mult)
+            nc.gpsimd.tensor_scalar(out=t1("negmu", r)[:], in0=sp[:, 0:1], scalar1=sp[:, 1:2], scalar2=-1.0 / H, op0=ALU.add, op1=ALU.mult)
 
         def Var(r):
             nc.scalar.activation(out=junk[:], in_=st[("pre", r)][:], func=ACT.Square, bias=st[("negmu", r)][:], accum_out=vs[:, r:r + 1])
 
-        def deviation(r, n):
-            nc.scalar.activation(out=std[:, r:r + n], in_=vs[:, r:r + n], func=ACT.Sqrt, scale=1.0 / H, bias=eps_ln[:])
+        def deviation(r):
+            nc.scalar.activation(out=t1("std", r)[:], in_=vs[:, r:r + 1], func=ACT.Sqrt, scale=1.0 / H, bias=eps_ln[:])
 
-        def rA(r, n):
-            nc.vector.reciprocal(out=rstd[:, r:r + n], in_=std[:, r:r + n])
+        def scale_a(r):
+            nc.vector.reciprocal(out=t1("rstd", r)[:], in_=st[("std", r)][:])
 
-        def rB(r, n):
-            nc.vector.tensor_tensor(out=rs[:, r:r + n], in0=rstd[:, r:r + n], in1=vec[:, 2 * HT + r:2 * HT + r + n], op=ALU.mult)
+        def scale_b(r):
+            t1("rs", r)
+            nc.vector.tensor_tensor(out=st[("rs", r)][:], in0=st[("rstd", r)][:], in1=s_col(r), op=ALU.mult)
+
+        def scale_last_two():
+            nc.gpsimd.tensor_scalar(out=var_g[:], in0=vs[:, 2:4], scalar1=1.0 / H, scalar2=1e-5, op0=ALU.mult, op1=ALU.add)
+            nc.gpsimd.tensor_tensor(out=rstd_g[:], in0=var_g[:], in1=inv_root[:], op=ALU.pow)
+            nc.gpsimd.tensor_tensor(out=rs_g[:], in0=rstd_g[:], in1=s_f[:, 2:4], op=ALU.mult)
+
+        def gain():
+            st["gain"] = bank(0, [P, H], "gain", BF16)
+            for j in range(HT):
+                nc.tensor.transpose(st["gain"][:, P * j:P * j + P], gain_col[:, j:j + 1].to_broadcast([P, P]), ident_bf[:])
 
         def I(r):
-            nc.vector.scalar_tensor_tensor(out=x1s[r][:], in0=st[("pre", r)][:], scalar=st[("negmu", r)][:], in1=g_bc, op0=ALU.add, op1=ALU.mult)
+            nc.vector.scalar_tensor_tensor(out=x1s[r][:], in0=st[("pre", r)][:], scalar=st[("negmu", r)][:], in1=st["gain"][:], op0=ALU.add, op1=ALU.mult)
 
         def R(r):
             rb = [bank(2 * r + hf, [P, 512], "rb") for hf in range(2)]
             for hf in range(2):
                 nc.tensor.matmul(out=rb[hf][:], lhsT=ident_bf[:], rhs=main_sb[:, r, half(hf)], start=True, stop=False)
                 nc.tensor.matmul(out=rb[hf][:], lhsT=dneg[r][:], rhs=main_sb[:, r, half(hf)], start=False, stop=False)
-                nc.tensor.matmul(out=rb[hf][:], lhsT=srow[:, P * r:P * r + P], rhs=brow[:, half(hf)], start=False, stop=True)
+                nc.tensor.matmul(out=rb[hf][:], lhsT=srow[:, r:B:RT], rhs=brow[:, half(hf)], start=False, stop=True)
             st[("rb", r)] = rb
 
         def K(r, hf):
             st[("sc", r)] = x1s[r]
-            q = st[("rb", r)][hf][:] if r in PE_BLEND else q3[:, half(hf)]
-            nc.vector.scalar_tensor_tensor(out=st[("sc", r)][:, half(hf)], in0=x1s[r][:, half(hf)], scalar=rs[:, r:r + 1], in1=q, op0=ALU.mult, op1=ALU.add)
+            q = st[("rb", r)][hf][:] if r in PE_BLEND else q0[:, half(hf)]
+            rs = rs_g[:, r - 2:r - 1] if r >= 2 else st[("rs", r)][:]
+            nc.vector.scalar_tensor_tensor(out=x1s[r][:, half(hf)], in0=x1s[r][:, half(hf)], scalar=rs, in1=q, op0=ALU.mult, op1=ALU.add)
 
         def store(dst, key, r, cols):
-            nc.sync.dma_start(out=dst[r * P:(r + 1) * P, cols], in_=st[(key, r)][:, cols])
+            nc.sync.dma_start(out=dst.rearrange("(p r) n -> p r n", r=RT)[:, r, cols], in_=st[(key, r)][:, cols])
 
         def tanh_table():
             nc.scalar.activation(out=warm[:, 1:2], in_=one1[:], func=ACT.Tanh)
 
         def L(r, cols):
             if ("th", r) not in st:
-                st[("th", r)] = work.tile([P, H], F32, name="th", bufs=4)
+                st[("th", r)] = work.tile([P, H], F32, name="th")
             nc.scalar.activation(out=st[("th", r)][:, cols], in_=st[("sc", r)][:, cols], func=ACT.Tanh)
 
         def M(r, cols, eng):
             eng.tensor_tensor(out=st[("th", r)][:, cols], in0=st[("th", r)][:, cols], in1=o_sb[:, r, cols], op=ALU.mult)
-            store(out_0, "th", r, cols)
 
         consts()
         small_loads()
@@ -295,27 +307,27 @@ def tile_bag_lstm_pb_kernel(tc, main, branch, o, is_bag, W_mb, b_mb, W_b, b_b, l
         load_rows(branch_sb, branch)
         load_chunk(2)
         load_chunk(3)
-        vec_cast()
-        vec_turn()
-        vec_copy()
         regroup(0, 0)
         regroup(0, 1)
         load_chunk(4)
-        blend_prep()
+        vec_cast()
         quantise(0, 0)
-        for c in range(2):
-            for rp in range(2):
-                turn_act(c, rp)
+        for rp in range(2):
+            turn_act(0, rp)
+        vec_turn()
+        for rp in range(2):
+            turn_act(1, rp)
         quantise(0, 1)
-        blend_term_a(3)
+        vec_copy()
+        blend_term_a()
         quantise_act(0)
-        regroup(1, 0)
-        quantise_act(1)
         main_norm(0)
         main_norm(1)
+        regroup(1, 0)
+        quantise_act(1)
         regroup(1, 1)
         load_chunk(5)
-        load_gb()
+        load_bias()
         load_rows(o_sb, o)
         quantise(1, 0)
         passes1(0, 0)
@@ -357,65 +369,85 @@ def tile_bag_lstm_pb_kernel(tc, main, branch, o, is_bag, W_mb, b_mb, W_b, b_b, l
         for j in range(4, HT):
             second_start(j)
             second_stop(j)
-        for r in range(2, RT):
-            main_norm(r)
-        n0()
+        main_norm(2)
+        main_norm(3)
+        main_root()
         for j in range(4):
             product(j, slice(0, B))
         for j in range(4, HT):
             product(j, slice(0, P))
         for j in range(4, HT):
             product(j, slice(P, B))
-        blend_term_b(3)
+        blend_term_b()
         for r in range(RT):
             turn_back(r)
-        D(0)
-        sq(0)
-        n4(0)
-        n5(0)
-        D(1)
-        sq(1)
-        for r in range(RT):
-            F(r, 0)
-            if r > 0:
-                nm(r - 1)
-            if r + 1 < RT:
-                n4(r + 1)
-            F(r, 1)
-            if r + 1 < RT:
-                n5(r + 1)
-            if r in PE_BLEND:
-                R(r)
-            if r + 2 < RT:
-                D(r + 2)
-                sq(r + 2)
-            if r > 0:
-                Var(r - 1)
-        deviation(0, 2)
-        nm(RT - 1)
+        for r in range(3):
+            D(r)
+            norm(r)
+        alpha_a(0)
+        alpha_b(0)
+        F(0, 0)
+        alpha_a(1)
+        F(0, 1)
+        alpha_b(1)
+        gain()
+        mean(0)
+        Var(0)
+        deviation(0)
+        D(3)
+        norm(3)
+        F(1, 0)
+        alpha_a(2)
+        F(1, 1)
+        alpha_b(2)
+        R(1)
+        mean(1)
+        Var(1)
+        deviation(1)
+        F(2, 0)
+        scale_a(0)
+        F(2, 1)
+        scale_b(0)
+        R(2)
+        mean(2)
+        Var(2)
         I(0)
-        rA(0, 2)
-        Var(RT - 1)
-        deviation(2, 2)
+        alpha_a(3)
+        K(0, 0)
+        alpha_b(3)
+        K(0, 1)
+        store(out_1, "sc", 0, whole)
+        F(3, 0)
+        scale_a(1)
+        F(3, 1)
+        scale_b(1)
+        R(3)
+        mean(3)
         tanh_table()
+        Var(3)
+        scale_last_two()
         I(1)
-        rB(0, 2)
-        for r in range(RT):
-            for hf in range(2):
-                K(r, hf)
-                if r == RT - 1:
-                    store(out_1, "sc", r, half(hf))
-                    L(r, half(hf))
-            if r < RT - 1:
-                store(out_1, "sc", r, whole)
-                L(r, whole)
-            if r == 0:
-                rA(2, 2)
-            if r + 2 < RT:
-                I(r + 2)
-            if r == 0:
-                rB(2, 2)
-        for r in range(RT - 1):
-            M(r, whole, nc.vector)
+        K(1, 0)
+        K(1, 1)
+        store(out_1, "sc", 1, whole)
+        L(0, whole)
+        L(1, whole)
+        I(2)
+        K(2, 0)
+        K(2, 1)
+        store(out_1, "sc", 2, whole)
+        L(2, whole)
         for hf in range(2):
-            M(RT - 1, half(hf), nc.vector)
+            M(0, half(hf), nc.gpsimd)
+        store(out_0, "th", 0, whole)
+        I(3)
+        for hf in range(2):
+            K(3, hf)
+            store(out_1, "sc", 3, half(hf))
+            L(3, half(hf))
+        for r in (1, 2):
+            M(r, whole, nc.vector)
+            store(out_0, "th", r, whole)
+        for hf in range(2):
+            M(3, half(hf), nc.vector)
+            store(out_0, "th", 3, half(hf))

@@ -55,6 +55,8 @@ def tile_bag_lstm_pb_kernel(tc, main, branch, o, is_bag, W_mb, b_mb, W_b, b_b, l
         o_sb = keep.tile([P, RT, H], BF16, name="o_sb")
         b_bc = keep.tile([P, H], BF16, name="b_bc")
         q0 = keep.tile([P, H], F32, name="q0")
+        qb = keep.tile([P, H], F32, name="qb")
+        late = keep.tile([P, 1], F32, name="late")
         dneg = {r: keep.tile([P, P], BF16, name="dneg%d" % r) for r in PE_BLEND}
         ags = [keep.tile([P, 2 * B], F32, name="ag%d" % c, align_bytes=64) for c in range(4)]
         aq = [keep.tile([P, B], U32, name="aq%d" % c, align_bytes=64) for c in range(4)]
@@ -67,10 +69,9 @@ def tile_bag_lstm_pb_kernel(tc, main, branch, o, is_bag, W_mb, b_mb, W_b, b_b, l
         em2 = keep.tile([P, RT], F32, name="em2")
         em = keep.tile([P, RT], F32, name="em")
         vs = keep.tile([P, RT], F32, name="vs")
-        inv_root = keep.tile([P, 2], F32, name="inv_root")
-        var_g = keep.tile([P, 2], F32, name="var_g")
-        rstd_g = keep.tile([P, 2], F32, name="rstd_g")
-        rs_g = keep.tile([P, 2], F32, name="rs_g")
+        inv_root = keep.tile([P, 1], F32, name="inv_root")
+        var_g = keep.tile([P, 1], F32, name="var_g")
+        rstd_g = keep.tile([P, 1], F32, name="rstd_g")
         junk = keep.tile([P, H], BF16, name="junk")
         raws = {}
         grps = {}
@@ -129,11 +130,13 @@ def tile_bag_lstm_pb_kernel(tc, main, branch, o, is_bag, W_mb, b_mb, W_b, b_b, l
             nc.tensor.transpose(st["vt"][:], vecs_f[:], ident[:])
 
         def vec_copy():
-            nc.vector.tensor_copy(out=s_f[:], in_=s_bf[:])
             nc.vector.tensor_copy(out=vec[:], in_=st["vt"][:, 0:3 * HT])
+            nc.vector.tensor_copy(out=gain_col[:], in_=st["vt"][:, 2 * HT:3 * HT])
+
+        def blend_prep():
+            nc.vector.tensor_copy(out=s_f[:], in_=s_bf[:])
             nc.vector.tensor_copy(out=ident_bf[:], in_=ident[:])
             nc.vector.tensor_scalar(out=oms[:], in0=s_f[:], scalar1=-1.0, scalar2=1.0, op0=ALU.mult, op1=ALU.add)
-            nc.vector.tensor_copy(out=gain_col[:], in_=vec[:, 2 * HT:3 * HT])
             for r in PE_BLEND:
                 nc.vector.tensor_scalar(out=dneg[r][:], in0=ident[:], scalar1=s_col(r), scalar2=-1.0, op0=ALU.mult, op1=ALU.mult)
 
@@ -141,7 +144,9 @@ def tile_bag_lstm_pb_kernel(tc, main, branch, o, is_bag, W_mb, b_mb, W_b, b_b, l
             nc.vector.tensor_scalar(out=q0[:], in0=main_sb[:, 0, :], scalar1=oms[:, 0:1], scalar2=None, op0=ALU.mult)
 
         def blend_term_b():
-            nc.vector.scalar_tensor_tensor(out=q0[:], in0=b_bc[:], scalar=s_col(0), in1=q0[:], op0=ALU.mult, op1=ALU.add)
+            nc.gpsimd.tensor_copy(out=late[:], in_=em[:, 0:1])
+            nc.gpsimd.tensor_scalar(out=qb[:], in0=b_bc[:], scalar1=s_col(0), scalar2=0.0, op0=ALU.mult, op1=ALU.add)
+            nc.gpsimd.tensor_tensor(out=q0[:], in0=q0[:], in1=qb[:], op=ALU.add)
 
         def turn_act(c, rp):
             src = main_sb if c < 2 else branch_sb
@@ -233,7 +238,8 @@ def tile_bag_lstm_pb_kernel(tc, main, branch, o, is_bag, W_mb, b_mb, W_b, b_b, l
             nc.vector.reciprocal(out=t1("rec", r)[:], in_=st[("den", r)][:])
 
         def alpha_b(r):
-            nc.vector.tensor_scalar(out=t1("alpha", r)[:], in0=st[("rec", r)][:], scalar1=em[:, r:r + 1], scalar2=1.0, op0=ALU.mult, op1=ALU.min)
+            eng = nc.gpsimd if r > 1 else nc.vector
+            eng.tensor_scalar(out=t1("alpha", r)[:], in0=st[("rec", r)][:], scalar1=em[:, r:r + 1], scalar2=1.0, op0=ALU.mult, op1=ALU.min)
 
         def F(r, hf):
             if hf == 0:
@@ -241,9 +247,9 @@ def tile_bag_lstm_pb_kernel(tc, main, branch, o, is_bag, W_mb, b_mb, W_b, b_b, l
                 t1("sp", r, 2)
             nc.vector.scalar_tensor_tensor(out=st[("pre", r)][:, half(hf)], in0=st[("hm", r)][hf][:], scalar=st[("alpha", r)][:], in1=main_sb[:, r, half(hf)], op0=ALU.mult, op1=ALU.add, accum_out=st[("sp", r)][:, hf:hf + 1])
 
-        def mean(r):
+        def mean(r, eng=nc.gpsimd):
             sp = st[("sp", r)]
-            nc.gpsimd.tensor_scalar(out=t1("negmu", r)[:], in0=sp[:, 0:1], scalar1=sp[:, 1:2], scalar2=-1.0 / H, op0=ALU.add, op1=ALU.mult)
+            eng.tensor_scalar(out=t1("negmu", r)[:], in0=sp[:, 0:1], scalar1=sp[:, 1:2], scalar2=-1.0 / H, op0=ALU.add, op1=ALU.mult)
 
         def Var(r):
             nc.scalar.activation(out=junk[:], in_=st[("pre", r)][:], func=ACT.Square, bias=st[("negmu", r)][:], accum_out=vs[:, r:r + 1])
@@ -256,12 +262,13 @@ def tile_bag_lstm_pb_kernel(tc, main, branch, o, is_bag, W_mb, b_mb, W_b, b_b, l
 
         def scale_b(r):
             t1("rs", r)
-            nc.vector.tensor_tensor(out=st[("rs", r)][:], in0=st[("rstd", r)][:], in1=s_col(r), op=ALU.mult)
+            nc.vector.tensor_scalar(out=st[("rs", r)][:], in0=st[("rstd", r)][:], scalar1=s_col(r), scalar2=None, op0=ALU.mult)
 
-        def scale_last_two():
-            nc.gpsimd.tensor_scalar(out=var_g[:], in0=vs[:, 2:4], scalar1=1.0 / H, scalar2=1e-5, op0=ALU.mult, op1=ALU.add)
+        def scale_last():
+            last = RT - 1
+            nc.gpsimd.tensor_scalar(out=var_g[:], in0=vs[:, last:last + 1], scalar1=1.0 / H, scalar2=1e-5, op0=ALU.mult, op1=ALU.add)
             nc.gpsimd.tensor_tensor(out=rstd_g[:], in0=var_g[:], in1=inv_root[:], op=ALU.pow)
-            nc.gpsimd.tensor_tensor(out=rs_g[:], in0=rstd_g[:], in1=s_f[:, 2:4], op=ALU.mult)
+            nc.gpsimd.tensor_tensor(out=t1("rs", last)[:], in0=rstd_g[:], in1=s_col(last), op=ALU.mult)
 
         def gain():
             st["gain"] = bank(0, [P, H], "gain", BF16)
@@ -282,8 +289,7 @@ def tile_bag_lstm_pb_kernel(tc, main, branch, o, is_bag, W_mb, b_mb, W_b, b_b, l
         def K(r, hf):
             st[("sc", r)] = x1s[r]
             q = st[("rb", r)][hf][:] if r in PE_BLEND else q0[:, half(hf)]
-            rs = rs_g[:, r - 2:r - 1] if r >= 2 else st[("rs", r)][:]
-            nc.vector.scalar_tensor_tensor(out=x1s[r][:, half(hf)], in0=x1s[r][:, half(hf)], scalar=rs, in1=q, op0=ALU.mult, op1=ALU.add)
+            nc.vector.scalar_tensor_tensor(out=x1s[r][:, half(hf)], in0=x1s[r][:, half(hf)], scalar=st[("rs", r)][:], in1=q, op0=ALU.mult, op1=ALU.add)
 
         def store(dst, key, r, cols):
             nc.sync.dma_start(out=dst.rearrange("(p r) n -> p r n", r=RT)[:, r, cols], in_=st[(key, r)][:, cols])
@@ -312,24 +318,25 @@ def tile_bag_lstm_pb_kernel(tc, main, branch, o, is_bag, W_mb, b_mb, W_b, b_b, l
         load_chunk(4)
         vec_cast()
         quantise(0, 0)
+        blend_prep()
         for rp in range(2):
             turn_act(0, rp)
         vec_turn()
         for rp in range(2):
             turn_act(1, rp)
         quantise(0, 1)
-        vec_copy()
         blend_term_a()
+        vec_copy()
         quantise_act(0)
         main_norm(0)
         main_norm(1)
         regroup(1, 0)
-        quantise_act(1)
         regroup(1, 1)
         load_chunk(5)
         load_bias()
         load_rows(o_sb, o)
         quantise(1, 0)
+        quantise_act(1)
         passes1(0, 0)
         for c in range(2, 4):
             for rp in range(2):
@@ -363,11 +370,13 @@ def tile_bag_lstm_pb_kernel(tc, main, branch, o, is_bag, W_mb, b_mb, W_b, b_b, l
             second_start(j)
         regroup(5, 1)
         quantise(5, 0)
+        second_start(4)
         for j in range(4):
             second_stop(j)
         quantise(5, 1)
-        for j in range(4, HT):
+        for j in range(5, HT):
             second_start(j)
+        for j in range(4, HT):
             second_stop(j)
         main_norm(2)
         main_norm(3)
@@ -394,8 +403,6 @@ def tile_bag_lstm_pb_kernel(tc, main, branch, o, is_bag, W_mb, b_mb, W_b, b_b, l
         mean(0)
         Var(0)
         deviation(0)
-        D(3)
-        norm(3)
         F(1, 0)
         alpha_a(2)
         F(1, 1)
@@ -404,6 +411,8 @@ def tile_bag_lstm_pb_kernel(tc, main, branch, o, is_bag, W_mb, b_mb, W_b, b_b, l
         mean(1)
         Var(1)
         deviation(1)
+        D(3)
+        norm(3)
         F(2, 0)
         scale_a(0)
         F(2, 1)
@@ -411,43 +420,47 @@ def tile_bag_lstm_pb_kernel(tc, main, branch, o, is_bag, W_mb, b_mb, W_b, b_b, l
         R(2)
         mean(2)
         Var(2)
+        deviation(2)
         I(0)
-        alpha_a(3)
+        scale_a(1)
         K(0, 0)
-        alpha_b(3)
+        scale_b(1)
         K(0, 1)
         store(out_1, "sc", 0, whole)
-        F(3, 0)
-        scale_a(1)
-        F(3, 1)
-        scale_b(1)
-        R(3)
-        mean(3)
         tanh_table()
-        Var(3)
-        scale_last_two()
+        L(0, whole)
         I(1)
+        alpha_a(3)
         K(1, 0)
+        alpha_b(3)
         K(1, 1)
         store(out_1, "sc", 1, whole)
-        L(0, whole)
         L(1, whole)
+        for hf in range(2):
+            M(0, half(hf), nc.gpsimd)
+        F(3, 0)
+        scale_a(2)
+        F(3, 1)
+        scale_b(2)
+        R(3)
         I(2)
+        mean(3, nc.vector)
+        Var(3)
+        scale_last()
         K(2, 0)
         K(2, 1)
         store(out_1, "sc", 2, whole)
         L(2, whole)
-        for hf in range(2):
-            M(0, half(hf), nc.gpsimd)
         store(out_0, "th", 0, whole)
         I(3)
+        M(1, whole, nc.vector)
+        store(out_0, "th", 1, whole)
         for hf in range(2):
             K(3, hf)
             store(out_1, "sc", 3, half(hf))
             L(3, half(hf))
-        for r in (1, 2):
-            M(r, whole, nc.vector)
-            store(out_0, "th", r, whole)
+        M(2, whole, nc.vector)
+        store(out_0, "th", 2, whole)
         for hf in range(2):
             M(3, half(hf), nc.vector)
             store(out_0, "th", 3, half(hf))

@@ -54,6 +54,7 @@ def tile_bag_lstm_pb_kernel(tc, main, branch, o, is_bag, W_mb, b_mb, W_b, b_b, l
         branch_sb = keep.tile([P, RT, H], BF16, name="branch_sb")
         o_sb = keep.tile([P, RT, H], BF16, name="o_sb")
         b_bc = keep.tile([P, H], BF16, name="b_bc")
+        g_bc = keep.tile([P, H], BF16, name="g_bc")
         q0 = keep.tile([P, H], F32, name="q0")
         qb = keep.tile([P, H], F32, name="qb")
         late = keep.tile([P, 1], F32, name="late")
@@ -121,6 +122,7 @@ def tile_bag_lstm_pb_kernel(tc, main, branch, o, is_bag, W_mb, b_mb, W_b, b_b, l
 
         def load_bias():
             nc.sync.dma_start(out=b_bc[:], in_=ln_b.partition_broadcast(P))
+            nc.sync.dma_start(out=g_bc[:], in_=ln_g.partition_broadcast(P))
 
         def vec_cast():
             nc.vector.tensor_copy(out=vecs_f[:], in_=vecs_bf[:])
@@ -238,8 +240,7 @@ def tile_bag_lstm_pb_kernel(tc, main, branch, o, is_bag, W_mb, b_mb, W_b, b_b, l
             nc.vector.reciprocal(out=t1("rec", r)[:], in_=st[("den", r)][:])
 
         def alpha_b(r):
-            eng = nc.gpsimd if r > 1 else nc.vector
-            eng.tensor_scalar(out=t1("alpha", r)[:], in0=st[("rec", r)][:], scalar1=em[:, r:r + 1], scalar2=1.0, op0=ALU.mult, op1=ALU.min)
+            nc.vector.tensor_scalar(out=t1("alpha", r)[:], in0=st[("rec", r)][:], scalar1=em[:, r:r + 1], scalar2=1.0, op0=ALU.mult, op1=ALU.min)
 
         def F(r, hf):
             if hf == 0:
@@ -274,6 +275,15 @@ def tile_bag_lstm_pb_kernel(tc, main, branch, o, is_bag, W_mb, b_mb, W_b, b_b, l
             st["gain"] = bank(0, [P, H], "gain", BF16)
             for j in range(HT):
                 nc.tensor.transpose(st["gain"][:, P * j:P * j + P], gain_col[:, j:j + 1].to_broadcast([P, P]), ident_bf[:])
+
+        def hold(r):
+            nc.gpsimd.tensor_copy(out=late[:], in_=x1s[r][:, H - 1:H])
+
+        def shifted(r):
+            nc.gpsimd.tensor_scalar(out=x1s[r][:], in0=st[("pre", r)][:], scalar1=st[("negmu", r)][:], scalar2=1.0, op0=ALU.add, op1=ALU.mult)
+
+        def gained(r):
+            nc.gpsimd.tensor_tensor(out=x1s[r][:], in0=x1s[r][:], in1=g_bc[:], op=ALU.mult)
 
         def I(r):
             nc.vector.scalar_tensor_tensor(out=x1s[r][:], in0=st[("pre", r)][:], scalar=st[("negmu", r)][:], in1=st["gain"][:], op0=ALU.add, op1=ALU.mult)
@@ -403,6 +413,7 @@ def tile_bag_lstm_pb_kernel(tc, main, branch, o, is_bag, W_mb, b_mb, W_b, b_b, l
         mean(0)
         Var(0)
         deviation(0)
+        shifted(0)
         F(1, 0)
         alpha_a(2)
         F(1, 1)
@@ -411,6 +422,7 @@ def tile_bag_lstm_pb_kernel(tc, main, branch, o, is_bag, W_mb, b_mb, W_b, b_b, l
         mean(1)
         Var(1)
         deviation(1)
+        gained(0)
         D(3)
         norm(3)
         F(2, 0)
@@ -421,44 +433,44 @@ def tile_bag_lstm_pb_kernel(tc, main, branch, o, is_bag, W_mb, b_mb, W_b, b_b, l
         mean(2)
         Var(2)
         deviation(2)
-        I(0)
+        I(1)
         scale_a(1)
         K(0, 0)
         scale_b(1)
         K(0, 1)
         store(out_1, "sc", 0, whole)
-        tanh_table()
-        L(0, whole)
-        I(1)
+        hold(0)
+        shifted(2)
+        gained(2)
         alpha_a(3)
         K(1, 0)
         alpha_b(3)
         K(1, 1)
         store(out_1, "sc", 1, whole)
-        L(1, whole)
-        for hf in range(2):
-            M(0, half(hf), nc.gpsimd)
         F(3, 0)
         scale_a(2)
         F(3, 1)
         scale_b(2)
         R(3)
-        I(2)
         mean(3, nc.vector)
+        tanh_table()
         Var(3)
         scale_last()
+        L(0, whole)
+        L(1, whole)
+        I(3)
         K(2, 0)
         K(2, 1)
         store(out_1, "sc", 2, whole)
         L(2, whole)
+        M(0, whole, nc.vector)
         store(out_0, "th", 0, whole)
-        I(3)
-        M(1, whole, nc.vector)
-        store(out_0, "th", 1, whole)
         for hf in range(2):
             K(3, hf)
             store(out_1, "sc", 3, half(hf))
             L(3, half(hf))
+        M(1, whole, nc.vector)
+        store(out_0, "th", 1, whole)
         M(2, whole, nc.vector)
         store(out_0, "th", 2, whole)
         for hf in range(2):

@@ -146,7 +146,7 @@ def tile_bag_lstm_pb_kernel(tc, main, branch, o, is_bag, W_mb, b_mb, W_b, b_b, l
             nc.vector.tensor_scalar(out=q0[:], in0=main_sb[:, 0, :], scalar1=oms[:, 0:1], scalar2=None, op0=ALU.mult)
 
         def blend_term_b():
-            nc.gpsimd.tensor_copy(out=late[:], in_=em[:, 0:1])
+            nc.gpsimd.tensor_copy(out=late[:], in_=hmT[0][:, 0:1])
             nc.gpsimd.tensor_scalar(out=qb[:], in0=b_bc[:], scalar1=s_col(0), scalar2=0.0, op0=ALU.mult, op1=ALU.add)
             nc.gpsimd.tensor_tensor(out=q0[:], in0=q0[:], in1=qb[:], op=ALU.add)
 
@@ -390,24 +390,25 @@ def tile_bag_lstm_pb_kernel(tc, main, branch, o, is_bag, W_mb, b_mb, W_b, b_b, l
             second_stop(j)
         main_norm(2)
         main_norm(3)
-        main_root()
         for j in range(4):
             product(j, slice(0, B))
+        blend_term_b()
         for j in range(4, HT):
             product(j, slice(0, P))
         for j in range(4, HT):
             product(j, slice(P, B))
-        blend_term_b()
         for r in range(RT):
             turn_back(r)
         for r in range(3):
             D(r)
+            if r == 0:
+                main_root()
             norm(r)
         alpha_a(0)
         alpha_b(0)
         F(0, 0)
-        alpha_a(1)
         F(0, 1)
+        alpha_a(1)
         alpha_b(1)
         gain()
         mean(0)
@@ -415,8 +416,8 @@ def tile_bag_lstm_pb_kernel(tc, main, branch, o, is_bag, W_mb, b_mb, W_b, b_b, l
         deviation(0)
         shifted(0)
         F(1, 0)
-        alpha_a(2)
         F(1, 1)
+        alpha_a(2)
         alpha_b(2)
         R(1)
         mean(1)
@@ -454,23 +455,23 @@ def tile_bag_lstm_pb_kernel(tc, main, branch, o, is_bag, W_mb, b_mb, W_b, b_b, l
         R(3)
         mean(3, nc.vector)
         tanh_table()
+        L(0, whole)
         Var(3)
         scale_last()
-        L(0, whole)
         L(1, whole)
         I(3)
+        M(0, whole, nc.vector)
+        store(out_0, "th", 0, whole)
         K(2, 0)
         K(2, 1)
         store(out_1, "sc", 2, whole)
         L(2, whole)
-        M(0, whole, nc.vector)
-        store(out_0, "th", 0, whole)
+        M(1, whole, nc.vector)
+        store(out_0, "th", 1, whole)
         for hf in range(2):
             K(3, hf)
             store(out_1, "sc", 3, half(hf))
             L(3, half(hf))
-        M(1, whole, nc.vector)
-        store(out_0, "th", 1, whole)
         M(2, whole, nc.vector)
         store(out_0, "th", 2, whole)
         for hf in range(2):

@@ -101,12 +101,14 @@ def tile_bag_lstm_pb_kernel(tc, main, branch, o, is_bag, W_mb, b_mb, W_b, b_b, l
             nc.gpsimd.memset(inv_root[:], -0.5)
 
         def small_loads():
-            for i, src in enumerate((b_mb, b_b, ln_g)):
-                nc.scalar.dma_start(out=vecs_bf[HT * i:HT * i + HT, :], in_=src.rearrange("(j p) -> j p", p=P))
-            nc.scalar.dma_start(out=s_bf[:], in_=is_bag.rearrange("(p r) a -> p (r a)", r=RT))
-            nc.scalar.dma_start(out=brow[0:1, :], in_=ln_b.rearrange("(a n) -> a n", a=1))
-            nc.scalar.dma_start(out=srow[0:1, :], in_=is_bag.rearrange("b a -> a b"))
+            nc.gpsimd.dma_start(out=brow[0:1, :], in_=ln_b.rearrange("(a n) -> a n", a=1))
+            nc.gpsimd.dma_start(out=srow[0:1, :], in_=is_bag.rearrange("b a -> a b"))
             nc.scalar.activation(out=warm[:, 0:1], in_=one1[:], func=ACT.Sqrt)
+
+        def vector_loads():
+            for i, src in enumerate((b_mb, b_b, ln_g)):
+                nc.sync.dma_start(out=vecs_bf[HT * i:HT * i + HT, :], in_=src.rearrange("(j p) -> j p", p=P))
+            nc.sync.dma_start(out=s_bf[:], in_=is_bag.rearrange("(p r) a -> p (r a)", r=RT))
 
         def load_rows(dst, src):
             rows = src.rearrange("(p r) n -> p r n", r=RT)
@@ -318,6 +320,7 @@ def tile_bag_lstm_pb_kernel(tc, main, branch, o, is_bag, W_mb, b_mb, W_b, b_b, l
         consts()
         small_loads()
         load_chunk(0)
+        vector_loads()
         load_rows(main_sb, main)
         load_chunk(1)
         load_rows(branch_sb, branch)

from contextlib import ExitStack

import concourse.mybir as mybir
from concourse.masks import make_identity

F32 = mybir.dt.float32
BF16 = mybir.dt.bfloat16
U32 = mybir.dt.uint32
U8 = mybir.dt.uint8
FP8X4 = mybir.dt.float8_e4m3fn_x4
ACT = mybir.ActivationFunctionType
ALU = mybir.AluOpType

P = 128
B = 512
H = 1024
RT = B // P
HT = H // P
FLOPS = 2 * B * (2 * H) * H + 2 * B * H * H
SCALAR_UNITS = ((0, 1), (2, 1), (3, 1), (4, 1))
PE_BLEND = (1, 2, 3)


def tile_bag_lstm_pb_kernel(tc, main, branch, o, is_bag, W_mb, b_mb, W_b, b_b, ln_g, ln_b, out_0, out_1):
    nc = tc.nc
    with ExitStack() as ctx:
        keep = ctx.enter_context(tc.tile_pool(name="keep", bufs=1))
        rawp = ctx.enter_context(tc.tile_pool(name="rawp", bufs=4))
        grpp = ctx.enter_context(tc.tile_pool(name="grpp", bufs=4))
        work = ctx.enter_context(tc.tile_pool(name="work", bufs=4))
        small = ctx.enter_context(tc.tile_pool(name="small", bufs=4))
        psum = ctx.enter_context(tc.psum_pool(name="psum", bufs=1))
        ctx.enter_context(tc.manual_schedule())

        def bank(i, shape, name, dtype=F32):
            return psum.tile(shape, dtype, tag="bank%d" % i, name=name)

        ident = keep.tile([P, P], F32, name="ident")
        ident_bf = keep.tile([P, P], BF16, name="ident_bf")
        vecs_bf = keep.tile([P, P], BF16, name="vecs_bf")
        vecs_f = keep.tile([P, P], F32, name="vecs_f")
        vec = keep.tile([P, 3 * HT], F32, name="vec")
        gain_col = keep.tile([P, HT], BF16, name="gain_col")
        s_bf = keep.tile([P, RT], BF16, name="s_bf")
        s_f = keep.tile([P, RT], F32, name="s_f")
        one1 = keep.tile([P, 1], F32, name="one1")
        eps_ln = keep.tile([P, 1], F32, name="eps_ln")
        eps_bag = keep.tile([P, 1], F32, name="eps_bag")
        warm = keep.tile([P, 2], F32, name="warm")
        brow = keep.tile([P, H], BF16, name="brow")
        srow = keep.tile([P, B], BF16, name="srow")
        oms = keep.tile([P, RT], F32, name="oms")
        main_sb = keep.tile([P, RT, H], BF16, name="main_sb")
        branch_sb = keep.tile([P, RT, H], BF16, name="branch_sb")
        o_sb = keep.tile([P, RT, H], BF16, name="o_sb")
        b_bc = keep.tile([P, H], BF16, name="b_bc")
        g_bc = keep.tile([P, H], BF16, name="g_bc")
        q0 = keep.tile([P, H], F32, name="q0")
        qb = keep.tile([P, H], F32, name="qb")
        late = keep.tile([P, 1], F32, name="late")
        dneg = {r: keep.tile([P, P], BF16, name="dneg%d" % r) for r in PE_BLEND}
        ags = [keep.tile([P, 2 * B], F32, name="ag%d" % c, align_bytes=64) for c in range(4)]
        aq = [keep.tile([P, B], U32, name="aq%d" % c, align_bytes=64) for c in range(4)]
        asc = [keep.tile([P, B], U8, name="as%d" % c, align_bytes=64) for c in range(4)]
        wq = [keep.tile([P, H], U32, name="wq%d" % c, align_bytes=64) for c in range(6)]
        ws = [keep.tile([P, H], U8, name="ws%d" % c, align_bytes=64) for c in range(6)]
        wbs = [keep.tile([P, B], F32, name="wb%d" % j) for j in range(HT)]
        hmT = [keep.tile([P, B], F32, name="hmT%d" % j) for j in range(HT)]
        x1s = [keep.tile([P, H], F32, name="x1_%d" % r) for r in range(RT)]
        em2 = keep.tile([P, RT], F32, name="em2")
        em = keep.tile([P, RT], F32, name="em")
        vs = keep.tile([P, RT], F32, name="vs")
        inv_root = keep.tile([P, 1], F32, name="inv_root")
        var_g = keep.tile([P, 1], F32, name="var_g")
        rstd_g = keep.tile([P, 1], F32, name="rstd_g")
        junk = keep.tile([P, H], BF16, name="junk")
        raws = {}
        grps = {}
        st = {}
        whole = slice(0, H)

        def half(hf):
            return slice(512 * hf, 512 * hf + 512)

        def s_col(r):
            return s_f[:, r:r + 1]

        def t1(key, r, w=1):
            t = small.tile([P, w], F32, name=key)
            st[(key, r)] = t
            return t

        def consts():
            make_identity(nc, ident[:])
            nc.vector.memset(vecs_bf[:], 0.0)
            nc.vector.memset(one1[:], 1.0)
            nc.vector.memset(brow[:], 0.0)
            nc.vector.memset(srow[:], 0.0)
            nc.vector.memset(eps_ln[:], 1e-5)
            nc.vector.memset(eps_bag[:], 1e-6)
            nc.gpsimd.memset(inv_root[:], -0.5)

        def small_loads():
            nc.gpsimd.dma_start(out=brow[0:1, :], in_=ln_b.rearrange("(a n) -> a n", a=1))
            nc.gpsimd.dma_start(out=srow[0:1, :], in_=is_bag.rearrange("b a -> a b"))
            nc.scalar.activation(out=warm[:, 0:1], in_=one1[:], func=ACT.Sqrt)

        def vector_loads():
            for i, src in enumerate((b_mb, b_b, ln_g)):
                nc.sync.dma_start(out=vecs_bf[HT * i:HT * i + HT, :], in_=src.rearrange("(j p) -> j p", p=P))
            nc.sync.dma_start(out=s_bf[:], in_=is_bag.rearrange("(p r) a -> p (r a)", r=RT))

        def load_rows(dst, src):
            rows = src.rearrange("(p r) n -> p r n", r=RT)
            for r in range(0, RT, 2):
                nc.sync.dma_start(out=dst[:, r:r + 2, :], in_=rows[:, r:r + 2, :])

        def load_chunk(c):
            w = W_mb if c < 4 else W_b
            k0 = 512 * (c % 4)
            raw = rawp.tile([P, 4, H], BF16, name="raw")
            nc.sync.dma_start(out=raw[:], in_=w[k0:k0 + 512, :].rearrange("(p t) n -> p t n", t=4))
            raws[c] = raw

        def load_bias():
            nc.sync.dma_start(out=b_bc[:], in_=ln_b.partition_broadcast(P))
            nc.sync.dma_start(out=g_bc[:], in_=ln_g.partition_broadcast(P))

        def vec_cast():
            nc.vector.tensor_copy(out=vecs_f[:], in_=vecs_bf[:])

        def vec_turn():
            st["vt"] = bank(3, [P, P], "vt")
            nc.tensor.transpose(st["vt"][:], vecs_f[:], ident[:])

        def vec_copy():
            nc.vector.tensor_copy(out=vec[:], in_=st["vt"][:, 0:3 * HT])
            nc.vector.tensor_copy(out=gain_col[:], in_=st["vt"][:, 2 * HT:3 * HT])

        def blend_prep():
            nc.vector.tensor_copy(out=s_f[:], in_=s_bf[:])
            nc.vector.tensor_copy(out=ident_bf[:], in_=ident[:])
            nc.vector.tensor_scalar(out=oms[:], in0=s_f[:], scalar1=-1.0, scalar2=1.0, op0=ALU.mult, op1=ALU.add)
            for r in PE_BLEND:
                nc.vector.tensor_scalar(out=dneg[r][:], in0=ident[:], scalar1=s_col(r), scalar2=-1.0, op0=ALU.mult, op1=ALU.mult)

        def blend_term_a():
            nc.vector.tensor_scalar(out=q0[:], in0=main_sb[:, 0, :], scalar1=oms[:, 0:1], scalar2=None, op0=ALU.mult)

        def blend_term_b():
            nc.gpsimd.tensor_copy(out=late[:], in_=hmT[0][:, 0:1])
            nc.gpsimd.tensor_scalar(out=qb[:], in0=b_bc[:], scalar1=s_col(0), scalar2=0.0, op0=ALU.mult, op1=ALU.add)
            nc.gpsimd.tensor_tensor(out=q0[:], in0=q0[:], in1=qb[:], op=ALU.add)

        def turn_act(c, rp):
            src = main_sb if c < 2 else branch_sb
            g = c % 2
            agv = ags[c][:].rearrange("p (b u) -> p b u", u=2)
            xt = bank(4 + (2 * c + rp) % 4, [P, 2, 2, P], "xt")
            for rr in range(2):
                words = src[:, 2 * rp + rr, :].bitcast(F32)
                for u in range(2):
                    nc.tensor.transpose(xt[:, rr, u, :], words[:, 256 * g + u:256 * g + 256:2], ident[:])
            nc.scalar.copy(
                out=agv[:, 256 * rp:256 * rp + 256, :].rearrange("p (rr b) u -> p rr b u", rr=2),
                in_=xt[:].rearrange("p rr u b -> p rr b u"),
            )

        def quantise_act(c):
            nc.vector.quantize_mx(out=aq[c][:].bitcast(FP8X4), scales=asc[c][:], in_=ags[c][:].bitcast(BF16))

        def regroup(c, hh):
            grp = grpp.tile([P, 512, 4], BF16, name="grp", align_bytes=64)
            dst = grp[:].rearrange("p (c i) t -> p c t i", i=8)
            srcv = raws[c][:, :, 512 * hh:512 * hh + 512].rearrange("p t (c i) -> p c t i", i=8)
            if (c, hh) in SCALAR_UNITS:
                nc.scalar.copy(out=dst, in_=srcv)
            else:
                nc.vector.tensor_copy(out=dst, in_=srcv)
            grps[(c, hh)] = grp

        def quantise(c, hh):
            nc.vector.quantize_mx(
                out=wq[c][:, 512 * hh:512 * hh + 512].bitcast(FP8X4),
                scales=ws[c][:, 512 * hh:512 * hh + 512],
                in_=grps[(c, hh)][:].rearrange("p w t -> p (w t)"),
            )

        def mx(acc, c, j, a, first, last):
            nc.tensor.matmul_mx(
                out=acc[:],
                lhsT=wq[c][:, P * j:P * j + P].bitcast(FP8X4),
                lhsT_scale=ws[c][:, P * j:P * j + P],
                rhs=aq[a][:].bitcast(FP8X4),
                rhs_scale=asc[a][:],
                start=first,
                stop=last,
            )

        def passes1(c, hh):
            for j in range(4 * hh, 4 * hh + 4):
                if c == 0:
                    st[("g1", j)] = bank(j, [P, B], "g1")
                mx(st[("g1", j)], c, j, c, c == 0, c == 3)

        def gate(j):
            nc.scalar.activation(out=wbs[j][:], in_=st[("g1", j)][:], func=ACT.Relu, bias=vec[:, j:j + 1])

        def main_norm(r):
            nc.scalar.activation(out=junk[:], in_=main_sb[:, r, :], func=ACT.Square, accum_out=em2[:, r:r + 1])

        def main_root():
            nc.scalar.activation(out=em[:], in_=em2[:], func=ACT.Sqrt)

        def second_start(j):
            st[("g2", j)] = bank(j, [P, B], "g2")
            mx(st[("g2", j)], 4, j, 2, True, False)

        def second_stop(j):
            mx(st[("g2", j)], 5, j, 3, False, True)

        def product(j, cols):
            nc.vector.scalar_tensor_tensor(out=hmT[j][:, cols], in0=st[("g2", j)][:, cols], scalar=vec[:, HT + j:HT + j + 1], in1=wbs[j][:, cols], op0=ALU.add, op1=ALU.mult)

        def turn_back(r):
            hm = [bank(2 * r + hf, [P, 512], "hm") for hf in range(2)]
            for j in range(HT):
                nc.tensor.transpose(hm[j // 4][:, P * (j % 4):P * (j % 4) + P], hmT[j][:, P * r:P * r + P], ident[:])
            st[("hm", r)] = hm

        def D(r):
            ssa = t1("ssa", r, 2)
            for hf in range(2):
                nc.scalar.activation(out=junk[:, 0:512], in_=st[("hm", r)][hf][:], func=ACT.Square, accum_out=ssa[:, hf:hf + 1])

        def norm(r):
            ssa = st[("ssa", r)]
            nc.scalar.activation(out=t1("nrm", r)[:], in_=ssa[:, 0:1], func=ACT.Sqrt, bias=ssa[:, 1:2])
            nc.scalar.activation(out=t1("den", r)[:], in_=st[("nrm", r)][:], func=ACT.Identity, bias=eps_bag[:])

        def alpha_a(r):
            nc.vector.reciprocal(out=t1("rec", r)[:], in_=st[("den", r)][:])

        def alpha_b(r):
            nc.vector.tensor_scalar(out=t1("alpha", r)[:], in0=st[("rec", r)][:], scalar1=em[:, r:r + 1], scalar2=1.0, op0=ALU.mult, op1=ALU.min)

        def F(r, hf):
            if hf == 0:
                st[("pre", r)] = work.tile([P, H], F32, name="pre")
                t1("sp", r, 2)
            nc.vector.scalar_tensor_tensor(out=st[("pre", r)][:, half(hf)], in0=st[("hm", r)][hf][:], scalar=st[("alpha", r)][:], in1=main_sb[:, r, half(hf)], op0=ALU.mult, op1=ALU.add, accum_out=st[("sp", r)][:, hf:hf + 1])

        def mean(r, eng=nc.gpsimd):
            sp = st[("sp", r)]
            eng.tensor_scalar(out=t1("negmu", r)[:], in0=sp[:, 0:1], scalar1=sp[:, 1:2], scalar2=-1.0 / H, op0=ALU.add, op1=ALU.mult)

        def Var(r):
            nc.scalar.activation(out=junk[:], in_=st[("pre", r)][:], func=ACT.Square, bias=st[("negmu", r)][:], accum_out=vs[:, r:r + 1])

        def deviation(r):
            nc.scalar.activation(out=t1("std", r)[:], in_=vs[:, r:r + 1], func=ACT.Sqrt, scale=1.0 / H, bias=eps_ln[:])

        def scale_a(r):
            nc.vector.reciprocal(out=t1("rstd", r)[:], in_=st[("std", r)][:])

        def scale_b(r):
            t1("rs", r)
            nc.vector.tensor_scalar(out=st[("rs", r)][:], in0=st[("rstd", r)][:], scalar1=s_col(r), scalar2=None, op0=ALU.mult)

        def scale_last():
            last = RT - 1
            nc.gpsimd.tensor_scalar(out=var_g[:], in0=vs[:, last:last + 1], scalar1=1.0 / H, scalar2=1e-5, op0=ALU.mult, op1=ALU.add)
            nc.gpsimd.tensor_tensor(out=rstd_g[:], in0=var_g[:], in1=inv_root[:], op=ALU.pow)
            nc.gpsimd.tensor_tensor(out=t1("rs", last)[:], in0=rstd_g[:], in1=s_col(last), op=ALU.mult)

        def gain():
            st["gain"] = bank(0, [P, H], "gain", BF16)
            for j in range(HT):
                nc.tensor.transpose(st["gain"][:, P * j:P * j + P], gain_col[:, j:j + 1].to_broadcast([P, P]), ident_bf[:])

        def hold(r):
            nc.gpsimd.tensor_copy(out=late[:], in_=x1s[r][:, H - 1:H])

        def shifted(r):
            nc.gpsimd.tensor_scalar(out=x1s[r][:], in0=st[("pre", r)][:], scalar1=st[("negmu", r)][:], scalar2=1.0, op0=ALU.add, op1=ALU.mult)

        def gained(r):
            nc.gpsimd.tensor_tensor(out=x1s[r][:], in0=x1s[r][:], in1=g_bc[:], op=ALU.mult)

        def I(r):
            nc.vector.scalar_tensor_tensor(out=x1s[r][:], in0=st[("pre", r)][:], scalar=st[("negmu", r)][:], in1=st["gain"][:], op0=ALU.add, op1=ALU.mult)

        def R(r):
            rb = [bank(2 * r + hf, [P, 512], "rb") for hf in range(2)]
            for hf in range(2):
                nc.tensor.matmul(out=rb[hf][:], lhsT=ident_bf[:], rhs=main_sb[:, r, half(hf)], start=True, stop=False)
                nc.tensor.matmul(out=rb[hf][:], lhsT=dneg[r][:], rhs=main_sb[:, r, half(hf)], start=False, stop=False)
                nc.tensor.matmul(out=rb[hf][:], lhsT=srow[:, r:B:RT], rhs=brow[:, half(hf)], start=False, stop=True)
            st[("rb", r)] = rb

        def K(r, hf):
            st[("sc", r)] = x1s[r]
            q = st[("rb", r)][hf][:] if r in PE_BLEND else q0[:, half(hf)]
            nc.vector.scalar_tensor_tensor(out=x1s[r][:, half(hf)], in0=x1s[r][:, half(hf)], scalar=st[("rs", r)][:], in1=q, op0=ALU.mult, op1=ALU.add)

        def store(dst, key, r, cols):
            nc.sync.dma_start(out=dst.rearrange("(p r) n -> p r n", r=RT)[:, r, cols], in_=st[(key, r)][:, cols])

        def tanh_table():
            nc.scalar.activation(out=warm[:, 1:2], in_=one1[:], func=ACT.Tanh)

        def L(r, cols):
            if ("th", r) not in st:
                st[("th", r)] = work.tile([P, H], F32, name="th")
            nc.scalar.activation(out=st[("th", r)][:, cols], in_=st[("sc", r)][:, cols], func=ACT.Tanh)

        def M(r, cols, eng):
            eng.tensor_tensor(out=st[("th", r)][:, cols], in0=st[("th", r)][:, cols], in1=o_sb[:, r, cols], op=ALU.mult)

        consts()
        small_loads()
        load_chunk(0)
        vector_loads()
        load_rows(main_sb, main)
        load_chunk(1)
        load_rows(branch_sb, branch)
        load_chunk(2)
        load_chunk(3)
        regroup(0, 0)
        regroup(0, 1)
        load_chunk(4)
        vec_cast()
        quantise(0, 0)
        blend_prep()
        for rp in range(2):
            turn_act(0, rp)
        vec_turn()
        for rp in range(2):
            turn_act(1, rp)
        quantise(0, 1)
        blend_term_a()
        vec_copy()
        quantise_act(0)
        main_norm(0)
        main_norm(1)
        regroup(1, 0)
        regroup(1, 1)
        load_chunk(5)
        load_bias()
        load_rows(o_sb, o)
        quantise(1, 0)
        quantise_act(1)
        passes1(0, 0)
        for c in range(2, 4):
            for rp in range(2):
                turn_act(c, rp)
        passes1(0, 1)
        passes1(1, 0)
        quantise(1, 1)
        passes1(1, 1)
        regroup(2, 0)
        quantise_act(2)
        regroup(2, 1)
        quantise(2, 0)
        quantise_act(3)
        passes1(2, 0)
        regroup(3, 0)
        regroup(3, 1)
        quantise(2, 1)
        passes1(2, 1)
        quantise(3, 0)
        passes1(3, 0)
        regroup(4, 0)
        regroup(4, 1)
        quantise(3, 1)
        passes1(3, 1)
        for j in range(HT):
            gate(j)
        quantise(4, 0)
        regroup(5, 0)
        quantise(4, 1)
        for j in range(4):
            second_start(j)
        regroup(5, 1)
        quantise(5, 0)
        second_start(4)
        for j in range(4):
            second_stop(j)
        quantise(5, 1)
        for j in range(5, HT):
            second_start(j)
        for j in range(4, HT):
            second_stop(j)
        main_norm(2)
        main_norm(3)
        for j in range(4):
            product(j, slice(0, B))
        blend_term_b()
        for j in range(4, HT):
            product(j, slice(0, P))
        for j in range(4, HT):
            product(j, slice(P, B))
        for r in range(RT):
            turn_back(r)
        for r in range(3):
            D(r)
            if r == 0:
                main_root()
            norm(r)
        alpha_a(0)
        alpha_b(0)
        F(0, 0)
        F(0, 1)
        alpha_a(1)
        alpha_b(1)
        gain()
        mean(0)
        Var(0)
        deviation(0)
        shifted(0)
        F(1, 0)
        F(1, 1)
        alpha_a(2)
        alpha_b(2)
        R(1)
        mean(1)
        Var(1)
        deviation(1)
        gained(0)
        D(3)
        norm(3)
        F(2, 0)
        scale_a(0)
        F(2, 1)
        scale_b(0)
        R(2)
        mean(2)
        Var(2)
        deviation(2)
        I(1)
        scale_a(1)
        K(0, 0)
        scale_b(1)
        K(0, 1)
        store(out_1, "sc", 0, whole)
        hold(0)
        shifted(2)
        gained(2)
        alpha_a(3)
        K(1, 0)
        alpha_b(3)
        K(1, 1)
        store(out_1, "sc", 1, whole)
        F(3, 0)
        scale_a(2)
        F(3, 1)
        scale_b(2)
        R(3)
        mean(3, nc.vector)
        tanh_table()
        L(0, whole)
        Var(3)
        scale_last()
        L(1, whole)
        I(3)
        M(0, whole, nc.vector)
        store(out_0, "th", 0, whole)
        K(2, 0)
        K(2, 1)
        store(out_1, "sc", 2, whole)
        L(2, whole)
        M(1, whole, nc.vector)
        store(out_0, "th", 1, whole)
        for hf in range(2):
            K(3, hf)
            store(out_1, "sc", 3, half(hf))
            L(3, half(hf))
        M(2, whole, nc.vector)
        store(out_0, "th", 2, whole)
        for hf in range(2):
            M(3, half(hf), nc.vector)
            store(out_0, "th", 3, half(hf))
